import numpy as np
import ml_dtypes


def mxq(x, axis, fmt="e4m3"):
    dtype, down = {"e4m3": (ml_dtypes.float8_e4m3fn, 7), "e5m2": (ml_dtypes.float8_e5m2, 14)}[fmt]
    v = np.moveaxis(np.asarray(x, np.float32).astype(ml_dtypes.bfloat16).astype(np.float64), axis, -1)
    blocks = v.reshape(v.shape[:-1] + (-1, 32))
    amax = np.abs(blocks).max(-1, keepdims=True)
    byte = np.maximum(np.where(amax > 0, np.frexp(amax)[1] - 1 + 127, 0) - down, 1)
    scale = np.exp2(byte - 127.0)
    codes = (blocks / scale).astype(np.float32).astype(dtype).astype(np.float64)
    return np.moveaxis((codes * scale).reshape(v.shape), -1, axis)


WIDE = False


def mx_kscale(k):
    if not WIDE:
        return np.ones(k)
    levels = np.array([10, -10, 5, -5, 0])
    a = np.random.permutation(np.resize(levels, k // 512 * 4)).reshape(k // 512, 4)
    idx = np.arange(k)
    return np.exp2(a[idx // 512, idx % 128 // 32])


BF16 = ml_dtypes.bfloat16


def bf(x):
    return np.asarray(x, np.float32).astype(BF16)


def f64(x):
    return np.asarray(x).astype(np.float64)


B, I, H = 8192, 512, 128
EPS = 1e-5


def sigmoid(v):
    return 1.0 / (1.0 + np.exp(-v))


def _bn(v, gamma, beta):
    m = np.mean(v, axis=0)
    var = np.var(v, axis=0)
    return (v - m) * (gamma / np.sqrt(var + EPS)) + beta


def setup_inputs():
    rn = np.random.standard_normal
    s = mx_kscale(I)
    return {"x": bf(rn((B, I)) * s),
            "c": bf(rn((B, H))),
            "h": bf(rn((B, H))),
            "w_ih": bf(rn((4 * H, I)) / np.sqrt(I) / s),
            "w_hh": bf(rn((4 * H, H)) / np.sqrt(H)),
            "b": bf(0.3 * rn(4 * H)),
            "g_ih": bf(1.0 + 0.1 * rn(4 * H)),
            "b_ih": bf(0.3 * rn(4 * H)),
            "g_hh": bf(1.0 + 0.1 * rn(4 * H)),
            "b_hh": bf(0.3 * rn(4 * H)),
            "g_c": bf(1.0 + 0.1 * rn(H)),
            "b_c": bf(0.3 * rn(H))}


def reference(x, c, h, w_ih, w_hh, b, g_ih, b_ih, g_hh, b_hh, g_c, b_c):
    ih = mxq(f64(x), 1, "e4m3") @ mxq(f64(w_ih), 1, "e4m3").T
    hh = f64(h) @ f64(w_hh).T
    ih = _bn(ih, f64(g_ih), f64(b_ih))
    hh = _bn(hh, f64(g_hh), f64(b_hh))
    gates = ih + hh + f64(b)
    f, i, o, g = np.split(gates, 4, axis=1)
    f = sigmoid(f)
    i = sigmoid(i)
    o = sigmoid(o)
    g = np.tanh(g)
    c_next = f * f64(c) + i * g
    c_next = _bn(c_next, f64(g_c), f64(b_c))
    h_next = o * np.tanh(c_next)
    return (c_next, h_next)

@@ -1,0 +1,329 @@
+from contextlib import ExitStack
+
+import concourse.mybir as mybir
+from concourse.masks import make_identity
+
+F32 = mybir.dt.float32
+BF16 = mybir.dt.bfloat16
+U32 = mybir.dt.uint32
+U8 = mybir.dt.uint8
+FP8X4 = mybir.dt.float8_e4m3fn_x4
+ACT = mybir.ActivationFunctionType
+ALU = mybir.AluOpType
+AX = mybir.AxisListType
+
+P = 128
+B, I, H = 8192, 512, 128
+NB = 4
+TILES = B // P
+TPC = 4
+CH = TILES // TPC
+CW = TPC * P
+EPS = 1e-5
+DIRECT = 2
+HG = 16
+FLOPS = 2 * B * I * NB * H + 2 * B * H * NB * H
+
+
+def tile_lstmcell_t_kernel(
+    tc, x, c, h, w_ih, w_hh, b, g_ih, b_ih, g_hh, b_hh, g_c, b_c, out_0, out_1
+):
+    nc = tc.nc
+    xv = x.rearrange("(p s) k -> p s k", s=TILES)
+    cv = c.rearrange("(p s) k -> p s k", s=TILES)
+    hv = h.rearrange("(p s) k -> p s k", s=TILES)
+    outv = (
+        out_0.rearrange("(p s) k -> p s k", s=TILES),
+        out_1.rearrange("(p s) k -> p s k", s=TILES),
+    )
+    with ExitStack() as ctx:
+        keep = ctx.enter_context(tc.tile_pool(name="keep", bufs=1))
+        psum = ctx.enter_context(tc.psum_pool(name="psum", bufs=1))
+        cpool = ctx.enter_context(tc.tile_pool(name="cpool", bufs=2))
+
+        gate = [keep.tile([P, B], F32, name="gate%d" % jb) for jb in range(NB)]
+        hT = keep.tile([P, B], BF16)
+        hh01 = keep.tile([P, NB, DIRECT, CW], F32)
+        w_codes = keep.tile([P, NB * P], U32, align_bytes=64)
+        w_scales = keep.tile([P, NB * P], U8, align_bytes=64)
+        whh_nat = keep.tile([P, NB, H], BF16)
+        whhT_b = keep.tile([P, NB * P], BF16)
+        whhT_f = keep.tile([P, NB * P], F32)
+        ident_f = keep.tile([P, P], F32)
+        ident_b = keep.tile([P, P], BF16)
+        rows = keep.tile([P, P], BF16)
+        par = keep.tile([P, 24], F32)
+        gs = keep.tile([P, P + 2], F32)
+        st_ih = keep.tile([P, NB, CH, 6], F32)
+        st_c = keep.tile([P, CH, 6], F32)
+        hsum = keep.tile([P, CH], F32)
+        sq01 = keep.tile([P, DIRECT, NB], F32)
+        junk = keep.tile([P, CW], F32)
+        prod = keep.tile([P, P], F32)
+        neghalf = keep.tile([P, NB], F32)
+        warm = keep.tile([P, 1], F32)
+
+        def small(name, width=NB):
+            return keep.tile([P, width], F32, name=name)
+
+        nc.vector.memset(warm[:], 0.0)
+        nc.scalar.activation(out=warm[:], in_=warm[:], func=ACT.Sigmoid)
+        nc.vector.memset(rows[:], 0.0)
+        nc.vector.memset(gs[:], 0.0)
+        nc.vector.memset(neghalf[:], -0.5)
+        make_identity(nc, ident_f[:])
+        make_identity(nc, ident_b[:])
+
+        with tc.tile_pool(name="stage", bufs=2) as stage:
+
+            def pack(src, codes, scales, on_scalar):
+                grp = stage.tile([P, 4 * CW], BF16, tag="grp", bufs=2, align_bytes=64, name="grp")
+                words = grp[:].bitcast(F32).rearrange("p (r u) -> p r u", u=2)
+                for half in range(2):
+                    xt = psum.tile([P, 2, 2 * P], F32, tag="tp", bufs=2, name="xt")
+                    for a in range(2):
+                        sw = src[:, 2 * half + a, :].bitcast(F32)
+                        for u in range(2):
+                            nc.tensor.transpose(
+                                xt[:, u, a * P : (a + 1) * P], sw[:, u * P : (u + 1) * P], ident_f[:]
+                            )
+                    dst = words[:, half * 2 * P : (half + 1) * 2 * P, :]
+                    srcv = xt[:].rearrange("p u r -> p r u")
+                    if on_scalar[half]:
+                        nc.scalar.copy(out=dst, in_=srcv)
+                    else:
+                        nc.vector.tensor_copy(out=dst, in_=srcv)
+                nc.vector.quantize_mx(out=codes.bitcast(FP8X4), scales=scales, in_=grp[:])
+
+            w_sb = stage.tile([P, NB, I], BF16, tag="xs", bufs=4, name="w_sb")
+            nc.sync.dma_start(out=w_sb[:], in_=w_ih.rearrange("(jb m) k -> m jb k", m=P))
+            x_sb = {}
+
+            def load_x(ci):
+                x_sb[ci] = stage.tile([P, TPC, I], BF16, tag="xs", bufs=4, name="x_sb")
+                nc.sync.dma_start(out=x_sb[ci][:], in_=xv[:, ci * TPC : (ci + 1) * TPC, :])
+
+            load_x(0)
+            load_x(1)
+            nc.sync.dma_start(out=whh_nat[:], in_=w_hh.rearrange("(jb m) k -> m jb k", m=P))
+            for v, vec in enumerate((b, g_ih, b_ih, g_hh, b_hh)):
+                nc.scalar.dma_start(
+                    out=rows[NB * v : NB * (v + 1), :], in_=vec.rearrange("(r m) -> r m", m=P)
+                )
+            nc.scalar.dma_start(out=rows[20:21, :], in_=g_c.rearrange("(r m) -> r m", m=P))
+            nc.scalar.dma_start(out=rows[21:22, :], in_=b_c.rearrange("(r m) -> r m", m=P))
+
+            pack(w_sb, w_codes[:], w_scales[:], (False, False))
+
+            gram = psum.tile([P, P], F32, tag="g", bufs=1, name="gram")
+            h_nat = {}
+            for ci in range(CH):
+                if ci + 2 < CH:
+                    load_x(ci + 2)
+                if ci % TPC == 0:
+                    hg = ci // TPC
+                    h_nat[hg] = stage.tile([P, HG, H], BF16, tag="hn", bufs=2, name="h_nat")
+                    nc.sync.dma_start(out=h_nat[hg][:], in_=hv[:, hg * HG : (hg + 1) * HG, :])
+                codes = stage.tile([P, CW], U32, tag="codes", bufs=2, align_bytes=64, name="codes")
+                scales = stage.tile([P, CW], U8, tag="scales", bufs=2, align_bytes=64, name="scales")
+                pack(x_sb[ci], codes[:], scales[:], (True, ci % 2 == 0))
+                cols = slice(ci * CW, (ci + 1) * CW)
+                for jb in range(NB):
+                    acc = psum.tile([P, CW], F32, tag="mm", bufs=5, name="acc")
+                    nc.tensor.matmul_mx(
+                        out=acc[:],
+                        lhsT=w_codes[:, jb * P : (jb + 1) * P].bitcast(FP8X4),
+                        lhsT_scale=w_scales[:, jb * P : (jb + 1) * P],
+                        rhs=codes[:].bitcast(FP8X4),
+                        rhs_scale=scales[:],
+                        start=True,
+                        stop=True,
+                    )
+                    nc.scalar.copy(out=gate[jb][:, cols], in_=acc[:])
+                    nc.vector.bn_stats(out=st_ih[:, jb, ci, :], in_=gate[jb][:, cols])
+
+                if ci == 0:
+                    wt = psum.tile([P, NB * P], BF16, tag="tp", bufs=2, name="wt")
+                    for jb in range(NB):
+                        nc.tensor.transpose(wt[:, jb * P : (jb + 1) * P], whh_nat[:, jb, :], ident_b[:])
+                    nc.vector.tensor_copy(out=whhT_b[:], in_=wt[:])
+                    nc.vector.tensor_copy(out=whhT_f[:], in_=wt[:])
+                    pt = psum.tile([P, P], BF16, tag="tp", bufs=2, name="pt")
+                    nc.tensor.transpose(pt[:], rows[:], ident_b[:])
+                    nc.vector.tensor_copy(out=par[:], in_=pt[:, 0:24])
+
+                hn = h_nat[ci // TPC]
+                ht = psum.tile([P, CW], BF16, tag="tp", bufs=2, name="ht")
+                for t in range(TPC):
+                    tt = (ci % TPC) * TPC + t
+                    nc.tensor.transpose(ht[:, t * P : (t + 1) * P], hn[:, tt, :], ident_b[:])
+                nc.scalar.activation(
+                    out=hT[:, cols], in_=ht[:], func=ACT.Copy, accum_out=hsum[:, ci : ci + 1]
+                )
+                if ci < DIRECT:
+                    for jb in range(NB):
+                        acc = psum.tile([P, CW], F32, tag="mm", bufs=5, name="acc")
+                        nc.tensor.matmul(
+                            out=acc[:],
+                            lhsT=whhT_b[:, jb * P : (jb + 1) * P],
+                            rhs=hT[:, cols],
+                            start=True,
+                            stop=True,
+                        )
+                        nc.scalar.activation(
+                            out=junk[:], in_=acc[:], func=ACT.Square,
+                            accum_out=sq01[:, ci, jb : jb + 1],
+                        )
+                        nc.scalar.copy(out=hh01[:, jb, ci, :], in_=acc[:])
+                else:
+                    for t in range(TPC):
+                        tt = (ci % TPC) * TPC + t
+                        nc.tensor.matmul(
+                            out=gram[:],
+                            lhsT=hn[:, tt, :],
+                            rhs=hn[:, tt, :],
+                            start=(ci == DIRECT and t == 0),
+                            stop=(ci == CH - 1 and t == TPC - 1),
+                        )
+
+        bsum = small("bsum")
+        nc.vector.tensor_tensor(out=bsum[:], in0=par[:, 0:4], in1=par[:, 8:12], op=ALU.add)
+        nc.vector.tensor_tensor(out=bsum[:], in0=bsum[:], in1=par[:, 16:20], op=ALU.add)
+        nc.vector.tensor_copy(out=gs[:, 0:P], in_=gram[:])
+        nc.vector.reduce_sum(out=gs[:, P : P + 1], in_=hsum[:], axis=AX.X)
+        t2 = small("t2")
+        s1 = small("s1")
+        for pair in range(2):
+            y = psum.tile([P, 2, P + 2], F32, tag="g", bufs=1, name="y")
+            for a in range(2):
+                jb = 2 * pair + a
+                nc.tensor.matmul(
+                    out=y[:, a, :], lhsT=whhT_f[:, jb * P : (jb + 1) * P], rhs=gs[:],
+                    start=True, stop=True,
+                )
+            for a in range(2):
+                jb = 2 * pair + a
+                nc.vector.tensor_tensor(out=prod[:], in0=y[:, a, 0:P], in1=whh_nat[:, jb, :], op=ALU.mult)
+                nc.vector.reduce_sum(out=t2[:, jb : jb + 1], in_=prod[:], axis=AX.X)
+                nc.vector.tensor_copy(out=s1[:, jb : jb + 1], in_=y[:, a, P : P + 1])
+        for ci in range(DIRECT):
+            nc.vector.tensor_tensor(out=t2[:], in0=t2[:], in1=sq01[:, ci, :], op=ALU.add)
+        mean_hh = small("mean_hh")
+        nc.vector.tensor_scalar(out=mean_hh[:], in0=s1[:], scalar1=1.0 / B, scalar2=None, op0=ALU.mult)
+        msq = small("msq")
+        nc.vector.tensor_tensor(out=msq[:], in0=mean_hh[:], in1=mean_hh[:], op=ALU.mult)
+        var_hh = small("var_hh")
+        nc.vector.scalar_tensor_tensor(
+            out=var_hh[:], in0=t2[:], scalar=1.0 / B, in1=msq[:], op0=ALU.mult, op1=ALU.subtract
+        )
+        nc.vector.tensor_scalar(
+            out=var_hh[:], in0=var_hh[:], scalar1=0.0, scalar2=EPS, op0=ALU.max, op1=ALU.add
+        )
+        rstd_hh = small("rstd_hh")
+        nc.gpsimd.tensor_tensor(out=rstd_hh[:], in0=var_hh[:], in1=neghalf[:], op=ALU.pow)
+        a_hh = small("a_hh")
+        nc.vector.tensor_tensor(out=a_hh[:], in0=par[:, 12:16], in1=rstd_hh[:], op=ALU.mult)
+        cst = small("cst")
+        nc.vector.tensor_tensor(out=cst[:], in0=a_hh[:], in1=mean_hh[:], op=ALU.mult)
+        nc.vector.tensor_tensor(out=cst[:], in0=bsum[:], in1=cst[:], op=ALU.subtract)
+
+        mv = keep.tile([P, NB, 2], F32)
+        for jb in range(NB):
+            nc.vector.bn_aggr(out=mv[:, jb, :], in_=st_ih[:, jb, :, :].rearrange("p c s -> p (c s)"))
+        ve_ih = small("ve_ih")
+        nc.vector.tensor_scalar(out=ve_ih[:], in0=mv[:, :, 1], scalar1=EPS, scalar2=None, op0=ALU.add)
+        rstd_ih = small("rstd_ih")
+        nc.gpsimd.tensor_tensor(out=rstd_ih[:], in0=ve_ih[:], in1=neghalf[:], op=ALU.pow)
+        a_ih = small("a_ih")
+        nc.vector.tensor_tensor(out=a_ih[:], in0=par[:, 4:8], in1=rstd_ih[:], op=ALU.mult)
+        zfix = small("zfix")
+        nc.vector.tensor_scalar(
+            out=zfix[:], in0=a_ih[:], scalar1=0.0, scalar2=1e-30, op0=ALU.is_equal, op1=ALU.mult
+        )
+        sc = small("sc")
+        nc.vector.tensor_tensor(out=sc[:], in0=a_ih[:], in1=zfix[:], op=ALU.add)
+        ratio = small("ratio")
+        nc.vector.reciprocal(out=ratio[:], in_=sc[:])
+        nc.vector.tensor_tensor(out=ratio[:], in0=ratio[:], in1=a_hh[:], op=ALU.mult)
+        am = small("am")
+        nc.vector.tensor_tensor(out=am[:], in0=a_ih[:], in1=mv[:, :, 0], op=ALU.mult)
+        nc.vector.tensor_tensor(out=cst[:], in0=cst[:], in1=am[:], op=ALU.subtract)
+
+        c_nat = {}
+        for ci in range(CH):
+            cols = slice(ci * CW, (ci + 1) * CW)
+            if ci % TPC == 0:
+                cg = ci // TPC
+                c_nat[cg] = cpool.tile([P, HG, H], BF16, tag="cn", bufs=2, name="c_nat")
+                nc.sync.dma_start(out=c_nat[cg][:], in_=cv[:, cg * HG : (cg + 1) * HG, :])
+            ct = psum.tile([P, CW], BF16, tag="tp", bufs=2, name="ct")
+            for t in range(TPC):
+                tt = (ci % TPC) * TPC + t
+                nc.tensor.transpose(ct[:, t * P : (t + 1) * P], c_nat[ci // TPC][:, tt, :], ident_b[:])
+            cT = cpool.tile([P, CW], BF16, tag="cT", bufs=3, name="cT")
+            nc.scalar.copy(out=cT[:], in_=ct[:])
+            for jb in range(NB):
+                if ci < DIRECT:
+                    hh = hh01[:, jb, ci, :]
+                else:
+                    acc = psum.tile([P, CW], F32, tag="mm", bufs=5, name="acc")
+                    nc.tensor.matmul(
+                        out=acc[:], lhsT=whhT_b[:, jb * P : (jb + 1) * P], rhs=hT[:, cols],
+                        start=True, stop=True,
+                    )
+                    hh = acc[:]
+                nc.vector.scalar_tensor_tensor(
+                    out=gate[jb][:, cols], in0=hh, scalar=ratio[:, jb : jb + 1], in1=gate[jb][:, cols],
+                    op0=ALU.mult, op1=ALU.add,
+                )
+                nc.scalar.activation(
+                    out=gate[jb][:, cols], in_=gate[jb][:, cols],
+                    func=(ACT.Tanh if jb == 3 else ACT.Sigmoid),
+                    scale=sc[:, jb : jb + 1], bias=cst[:, jb : jb + 1],
+                )
+            nc.gpsimd.tensor_tensor(out=gate[0][:, cols], in0=gate[0][:, cols], in1=cT[:], op=ALU.mult)
+            nc.gpsimd.tensor_tensor(
+                out=gate[1][:, cols], in0=gate[1][:, cols], in1=gate[3][:, cols], op=ALU.mult
+            )
+            nc.vector.tensor_tensor(
+                out=gate[0][:, cols], in0=gate[0][:, cols], in1=gate[1][:, cols], op=ALU.add
+            )
+            nc.vector.bn_stats(out=st_c[:, ci, :], in_=gate[0][:, cols])
+
+        mvc = keep.tile([P, 2], F32)
+        nc.vector.bn_aggr(out=mvc[:], in_=st_c[:].rearrange("p c s -> p (c s)"))
+        ve_c = small("ve_c", 1)
+        nc.vector.tensor_scalar(out=ve_c[:], in0=mvc[:, 1:2], scalar1=EPS, scalar2=None, op0=ALU.add)
+        rstd_c = small("rstd_c", 1)
+        nc.gpsimd.tensor_tensor(out=rstd_c[:], in0=ve_c[:], in1=neghalf[:, 0:1], op=ALU.pow)
+        a_c = small("a_c", 1)
+        nc.vector.tensor_tensor(out=a_c[:], in0=par[:, 20:21], in1=rstd_c[:], op=ALU.mult)
+        k_c = small("k_c", 1)
+        nc.vector.tensor_tensor(out=k_c[:], in0=a_c[:], in1=mvc[:, 0:1], op=ALU.mult)
+        nc.vector.tensor_tensor(out=k_c[:], in0=par[:, 21:22], in1=k_c[:], op=ALU.subtract)
+
+        with tc.tile_pool(name="outs", bufs=3) as outs:
+            for ci in range(CH):
+                cols = slice(ci * CW, (ci + 1) * CW)
+                nc.vector.tensor_scalar(
+                    out=gate[1][:, cols], in0=gate[0][:, cols], scalar1=a_c[:], scalar2=k_c[:],
+                    op0=ALU.mult, op1=ALU.add,
+                )
+                nc.scalar.activation(
+                    out=gate[3][:, cols], in_=gate[0][:, cols], func=ACT.Tanh, scale=a_c[:], bias=k_c[:]
+                )
+                nc.vector.tensor_tensor(
+                    out=gate[2][:, cols], in0=gate[2][:, cols], in1=gate[3][:, cols], op=ALU.mult
+                )
+                for o, src in enumerate((gate[1], gate[2])):
+                    ot = psum.tile([P, TPC, P], F32, tag="mm", bufs=5, name="ot")
+                    for t in range(TPC):
+                        nc.tensor.transpose(
+                            ot[:, t, :], src[:, ci * CW + t * P : ci * CW + (t + 1) * P], ident_f[:]
+                        )
+                    ob = outs.tile([P, TPC, P], F32, tag="ob%d" % o, bufs=3, name="ob")
+                    if o == 0:
+                        nc.scalar.copy(out=ob[:], in_=ot[:])
+                    else:
+                        nc.vector.tensor_copy(out=ob[:], in_=ot[:])
+                    nc.sync.dma_start(out=outv[o][:, ci * TPC : (ci + 1) * TPC, :], in_=ob[:])

@@ -22,6 +22,10 @@ CW = TPC * P
 EPS = 1e-5
 DIRECT = 2
 HG = 16
+HPAD = 144
+GW = P + 2
+OLAG = 6
+CFILL = 8
 FLOPS = 2 * B * I * NB * H + 2 * B * H * NB * H
 
 
@@ -37,6 +41,7 @@ def tile_lstmcell_t_kernel(
         out_1.rearrange("(p s) k -> p s k", s=TILES),
     )
     with ExitStack() as ctx:
+        ctx.enter_context(tc.manual_schedule())
         keep = ctx.enter_context(tc.tile_pool(name="keep", bufs=1))
         psum = ctx.enter_context(tc.psum_pool(name="psum", bufs=1))
         cpool = ctx.enter_context(tc.tile_pool(name="cpool", bufs=2))
@@ -44,6 +49,7 @@ def tile_lstmcell_t_kernel(
         gate = [keep.tile([P, B], F32, name="gate%d" % jb) for jb in range(NB)]
         hT = keep.tile([P, B], BF16)
         hh01 = keep.tile([P, NB, DIRECT, CW], F32)
+        h_nat = [keep.tile([P, HG, HPAD], BF16, name="h_nat%d" % g) for g in range(TILES // HG)]
         w_codes = keep.tile([P, NB * P], U32, align_bytes=64)
         w_scales = keep.tile([P, NB * P], U8, align_bytes=64)
         whh_nat = keep.tile([P, NB, H], BF16)
@@ -53,181 +59,277 @@ def tile_lstmcell_t_kernel(
         ident_b = keep.tile([P, P], BF16)
         rows = keep.tile([P, P], BF16)
         par = keep.tile([P, 24], F32)
-        gs = keep.tile([P, P + 2], F32)
+        gs = keep.tile([P, GW], F32)
         st_ih = keep.tile([P, NB, CH, 6], F32)
-        st_c = keep.tile([P, CH, 6], F32)
-        hsum = keep.tile([P, CH], F32)
+        hsum = keep.tile([P, DIRECT], F32)
         sq01 = keep.tile([P, DIRECT, NB], F32)
-        junk = keep.tile([P, CW], F32)
+        csum = keep.tile([P, CH], F32)
+        csq = keep.tile([P, CH], F32)
+        junk = keep.tile([P, CW], BF16)
         prod = keep.tile([P, P], F32)
         neghalf = keep.tile([P, NB], F32)
         warm = keep.tile([P, 1], F32)
+        mv = keep.tile([P, NB, 2], F32)
 
         def small(name, width=NB):
             return keep.tile([P, width], F32, name=name)
 
+        def cols(ci):
+            return slice(ci * CW, (ci + 1) * CW)
+
+        def blk(jb):
+            return slice(jb * P, (jb + 1) * P)
+
+        def htile(ci, t):
+            s = ci * TPC + t
+            return h_nat[s // HG][:, s % HG, :]
+
+        def transpose_bf16(tag, tiles):
+            bank = psum.tile([P, CW], BF16, tag=tag, name="bt")
+            for t, src in enumerate(tiles):
+                nc.tensor.transpose(bank[:, t * P : (t + 1) * P], src, ident_b[:])
+            return bank
+
+        def hh_matmul(ci, jb):
+            acc = psum.tile([P, CW], F32, tag="m%d" % jb, name="acc")
+            nc.tensor.matmul(out=acc[:], lhsT=whhT_b[:, blk(jb)], rhs=hT[:, cols(ci)], start=True, stop=True)
+            return acc
+
         nc.vector.memset(warm[:], 0.0)
         nc.scalar.activation(out=warm[:], in_=warm[:], func=ACT.Sigmoid)
-        nc.vector.memset(rows[:], 0.0)
-        nc.vector.memset(gs[:], 0.0)
-        nc.vector.memset(neghalf[:], -0.5)
         make_identity(nc, ident_f[:])
         make_identity(nc, ident_b[:])
+        nc.vector.memset(rows[:], 0.0)
+        nc.vector.memset(neghalf[:], -0.5)
+        for g in range(TILES // HG):
+            nc.vector.memset(h_nat[g][:, :, H:HPAD], 1.0)
 
         with tc.tile_pool(name="stage", bufs=2) as stage:
+            x_sb = {}
+            banks = {}
+            grp = {}
+            codes = {}
+            scales = {}
+            acc_ih = {}
 
-            def pack(src, codes, scales, on_scalar):
-                grp = stage.tile([P, 4 * CW], BF16, tag="grp", bufs=2, align_bytes=64, name="grp")
-                words = grp[:].bitcast(F32).rearrange("p (r u) -> p r u", u=2)
-                for half in range(2):
-                    xt = psum.tile([P, 2, 2 * P], F32, tag="tp", bufs=2, name="xt")
+            def load_x(ci):
+                x_sb[ci] = stage.tile([P, TPC, I], BF16, tag="xs", bufs=4, name="x_sb")
+                nc.sync.dma_start(out=x_sb[ci][:], in_=xv[:, ci * TPC : (ci + 1) * TPC, :])
+
+            def load_h(g):
+                nc.sync.dma_start(out=h_nat[g][:, :, 0:H], in_=hv[:, g * HG : (g + 1) * HG, :])
+
+            def t1(key, src, tags=("ta", "tb")):
+                pair = []
+                for half, tag in enumerate(tags):
+                    xt = psum.tile([P, 2, 2 * P], F32, tag=tag, name="xt")
                     for a in range(2):
                         sw = src[:, 2 * half + a, :].bitcast(F32)
                         for u in range(2):
                             nc.tensor.transpose(
                                 xt[:, u, a * P : (a + 1) * P], sw[:, u * P : (u + 1) * P], ident_f[:]
                             )
-                    dst = words[:, half * 2 * P : (half + 1) * 2 * P, :]
-                    srcv = xt[:].rearrange("p u r -> p r u")
-                    if on_scalar[half]:
-                        nc.scalar.copy(out=dst, in_=srcv)
-                    else:
-                        nc.vector.tensor_copy(out=dst, in_=srcv)
-                nc.vector.quantize_mx(out=codes.bitcast(FP8X4), scales=scales, in_=grp[:])
+                    pair.append(xt)
+                banks[key] = pair
+
+            def new_grp(key):
+                grp[key] = stage.tile([P, 4 * CW], BF16, tag="grp", bufs=2, align_bytes=64, name="grp")
+
+            def evac(key, half, on_scalar):
+                words = grp[key][:].bitcast(F32).rearrange("p (r u) -> p r u", u=2)
+                dst = words[:, half * 2 * P : (half + 1) * 2 * P, :]
+                src = banks[key][half][:].rearrange("p u r -> p r u")
+                if on_scalar:
+                    nc.scalar.copy(out=dst, in_=src)
+                else:
+                    nc.vector.tensor_copy(out=dst, in_=src)
+
+            def quant(key):
+                codes[key] = stage.tile([P, CW], U32, tag="codes", bufs=2, align_bytes=64, name="codes")
+                scales[key] = stage.tile([P, CW], U8, tag="scales", bufs=2, align_bytes=64, name="scales")
+                nc.vector.quantize_mx(
+                    out=codes[key][:].bitcast(FP8X4), scales=scales[key][:], in_=grp[key][:]
+                )
+
+            def mx(ci):
+                acc_ih[ci] = []
+                for jb in range(NB):
+                    acc = psum.tile([P, CW], F32, tag="m%d" % jb, name="acc")
+                    nc.tensor.matmul_mx(
+                        out=acc[:],
+                        lhsT=w_codes[:, blk(jb)].bitcast(FP8X4),
+                        lhsT_scale=w_scales[:, blk(jb)],
+                        rhs=codes[ci][:].bitcast(FP8X4),
+                        rhs_scale=scales[ci][:],
+                        start=True,
+                        stop=True,
+                    )
+                    acc_ih[ci].append(acc)
+
+            def copy_ih(ci):
+                for jb in range(NB):
+                    nc.scalar.copy(out=gate[jb][:, cols(ci)], in_=acc_ih[ci][jb][:])
+
+            def stat_ih(ci, jb):
+                nc.vector.bn_stats(out=st_ih[:, jb, ci, :], in_=gate[jb][:, cols(ci)])
+
+            def v_takes_half(ci):
+                return ci % 4 == 1
 
             w_sb = stage.tile([P, NB, I], BF16, tag="xs", bufs=4, name="w_sb")
             nc.sync.dma_start(out=w_sb[:], in_=w_ih.rearrange("(jb m) k -> m jb k", m=P))
-            x_sb = {}
-
-            def load_x(ci):
-                x_sb[ci] = stage.tile([P, TPC, I], BF16, tag="xs", bufs=4, name="x_sb")
-                nc.sync.dma_start(out=x_sb[ci][:], in_=xv[:, ci * TPC : (ci + 1) * TPC, :])
-
             load_x(0)
             load_x(1)
-            nc.sync.dma_start(out=whh_nat[:], in_=w_hh.rearrange("(jb m) k -> m jb k", m=P))
+            load_x(2)
             for v, vec in enumerate((b, g_ih, b_ih, g_hh, b_hh)):
                 nc.scalar.dma_start(
                     out=rows[NB * v : NB * (v + 1), :], in_=vec.rearrange("(r m) -> r m", m=P)
                 )
             nc.scalar.dma_start(out=rows[20:21, :], in_=g_c.rearrange("(r m) -> r m", m=P))
             nc.scalar.dma_start(out=rows[21:22, :], in_=b_c.rearrange("(r m) -> r m", m=P))
+            nc.sync.dma_start(out=whh_nat[:], in_=w_hh.rearrange("(jb m) k -> m jb k", m=P))
 
-            pack(w_sb, w_codes[:], w_scales[:], (False, False))
+            t1("w", w_sb)
+            load_x(3)
+            load_h(0)
+            t1(0, x_sb[0], ("th", "g"))
+            load_x(4)
+            new_grp("w")
+            evac("w", 0, True)
+            evac("w", 1, False)
+            nc.vector.quantize_mx(out=w_codes[:].bitcast(FP8X4), scales=w_scales[:], in_=grp["w"][:])
+            new_grp(0)
+            evac(0, 0, True)
+            evac(0, 1, False)
+            quant(0)
+            t1(1, x_sb[1])
+            load_x(5)
+            mx(0)
 
-            gram = psum.tile([P, P], F32, tag="g", bufs=1, name="gram")
-            h_nat = {}
+            c_nat = {}
+
+            def load_c(cg):
+                c_nat[cg] = cpool.tile([P, HG, H], BF16, tag="cn", bufs=2, name="c_nat")
+                nc.sync.dma_start(out=c_nat[cg][:], in_=cv[:, cg * HG : (cg + 1) * HG, :])
+
+            gram = None
             for ci in range(CH):
+                nxt = ci + 1
+                if nxt < CH:
+                    new_grp(nxt)
+                    evac(nxt, 0, True)
+                    if not v_takes_half(nxt):
+                        evac(nxt, 1, True)
+                if ci >= 1:
+                    for jb in range(3):
+                        stat_ih(ci - 1, jb)
+                if nxt < CH and v_takes_half(nxt):
+                    evac(nxt, 1, False)
+                if ci >= 1:
+                    stat_ih(ci - 1, 3)
+                if nxt < CH:
+                    quant(nxt)
                 if ci + 2 < CH:
-                    load_x(ci + 2)
-                if ci % TPC == 0:
-                    hg = ci // TPC
-                    h_nat[hg] = stage.tile([P, HG, H], BF16, tag="hn", bufs=2, name="h_nat")
-                    nc.sync.dma_start(out=h_nat[hg][:], in_=hv[:, hg * HG : (hg + 1) * HG, :])
-                codes = stage.tile([P, CW], U32, tag="codes", bufs=2, align_bytes=64, name="codes")
-                scales = stage.tile([P, CW], U8, tag="scales", bufs=2, align_bytes=64, name="scales")
-                pack(x_sb[ci], codes[:], scales[:], (True, ci % 2 == 0))
-                cols = slice(ci * CW, (ci + 1) * CW)
-                for jb in range(NB):
-                    acc = psum.tile([P, CW], F32, tag="mm", bufs=5, name="acc")
-                    nc.tensor.matmul_mx(
-                        out=acc[:],
-                        lhsT=w_codes[:, jb * P : (jb + 1) * P].bitcast(FP8X4),
-                        lhsT_scale=w_scales[:, jb * P : (jb + 1) * P],
-                        rhs=codes[:].bitcast(FP8X4),
-                        rhs_scale=scales[:],
-                        start=True,
-                        stop=True,
-                    )
-                    nc.scalar.copy(out=gate[jb][:, cols], in_=acc[:])
-                    nc.vector.bn_stats(out=st_ih[:, jb, ci, :], in_=gate[jb][:, cols])
-
+                    t1(ci + 2, x_sb[ci + 2])
+                    if ci + 6 < CH:
+                        load_x(ci + 6)
+                if ci in (0, 2, 4):
+                    load_h(ci // 2 + 1)
+                if ci in (8, 9):
+                    load_c(ci - 8)
                 if ci == 0:
-                    wt = psum.tile([P, NB * P], BF16, tag="tp", bufs=2, name="wt")
-                    for jb in range(NB):
-                        nc.tensor.transpose(wt[:, jb * P : (jb + 1) * P], whh_nat[:, jb, :], ident_b[:])
+                    wt = transpose_bf16("g", [whh_nat[:, jb, :] for jb in range(NB)])
                     nc.vector.tensor_copy(out=whhT_b[:], in_=wt[:])
                     nc.vector.tensor_copy(out=whhT_f[:], in_=wt[:])
-                    pt = psum.tile([P, P], BF16, tag="tp", bufs=2, name="pt")
+                    pt = psum.tile([P, P], BF16, tag="th", name="pt")
                     nc.tensor.transpose(pt[:], rows[:], ident_b[:])
                     nc.vector.tensor_copy(out=par[:], in_=pt[:, 0:24])
-
-                hn = h_nat[ci // TPC]
-                ht = psum.tile([P, CW], BF16, tag="tp", bufs=2, name="ht")
-                for t in range(TPC):
-                    tt = (ci % TPC) * TPC + t
-                    nc.tensor.transpose(ht[:, t * P : (t + 1) * P], hn[:, tt, :], ident_b[:])
-                nc.scalar.activation(
-                    out=hT[:, cols], in_=ht[:], func=ACT.Copy, accum_out=hsum[:, ci : ci + 1]
-                )
-                if ci < DIRECT:
-                    for jb in range(NB):
-                        acc = psum.tile([P, CW], F32, tag="mm", bufs=5, name="acc")
-                        nc.tensor.matmul(
-                            out=acc[:],
-                            lhsT=whhT_b[:, jb * P : (jb + 1) * P],
-                            rhs=hT[:, cols],
-                            start=True,
-                            stop=True,
-                        )
+                copy_ih(ci)
+                if ci == 1:
+                    for q, tag in enumerate(("th", "g")):
+                        ht = transpose_bf16(tag, [htile(q, t)[:, 0:H] for t in range(TPC)])
                         nc.scalar.activation(
-                            out=junk[:], in_=acc[:], func=ACT.Square,
-                            accum_out=sq01[:, ci, jb : jb + 1],
+                            out=hT[:, cols(q)], in_=ht[:], func=ACT.Copy, accum_out=hsum[:, q : q + 1]
                         )
-                        nc.scalar.copy(out=hh01[:, jb, ci, :], in_=acc[:])
-                else:
-                    for t in range(TPC):
-                        tt = (ci % TPC) * TPC + t
-                        nc.tensor.matmul(
-                            out=gram[:],
-                            lhsT=hn[:, tt, :],
-                            rhs=hn[:, tt, :],
-                            start=(ci == DIRECT and t == 0),
-                            stop=(ci == CH - 1 and t == TPC - 1),
+                if 3 <= ci <= 9:
+                    if ci == 3:
+                        gram = psum.tile([P, GW], F32, tag="g", name="gram")
+                    for q in (2 * ci - 4, 2 * ci - 3):
+                        for t in range(TPC):
+                            nc.tensor.matmul(
+                                out=gram[:],
+                                lhsT=htile(q, t)[:, 0:H],
+                                rhs=htile(q, t)[:, 0:GW],
+                                start=(q == DIRECT and t == 0),
+                                stop=(q == CH - 1 and t == TPC - 1),
+                            )
+                if ci in (2, 5):
+                    q = (ci - 2) // 3
+                    for jb in range(NB):
+                        acc = hh_matmul(q, jb)
+                        nc.vector.tensor_copy(out=hh01[:, jb, q, :], in_=acc[:])
+                        nc.scalar.activation(
+                            out=junk[:], in_=acc[:], func=ACT.Square, accum_out=sq01[:, q, jb : jb + 1]
                         )
+                if nxt < CH:
+                    mx(nxt)
+                if ci == 10:
+                    nc.vector.tensor_copy(out=gs[:], in_=gram[:])
+                    for q in range(DIRECT):
+                        nc.vector.tensor_tensor(
+                            out=gs[:, P : P + 1], in0=gs[:, P : P + 1], in1=hsum[:, q : q + 1], op=ALU.add
+                        )
+                    ys = []
+                    for pair, tag in enumerate(("th", "g")):
+                        y = psum.tile([P, 2, GW], F32, tag=tag, name="y")
+                        for a in range(2):
+                            nc.tensor.matmul(
+                                out=y[:, a, :], lhsT=whhT_f[:, blk(2 * pair + a)], rhs=gs[:],
+                                start=True, stop=True,
+                            )
+                        ys.append(y)
+                if ci == 11:
+                    t2 = small("t2")
+                    s1 = small("s1")
+                    for jb in range(NB):
+                        y = ys[jb // 2]
+                        a = jb % 2
+                        nc.vector.tensor_tensor(
+                            out=prod[:], in0=y[:, a, 0:P], in1=whh_nat[:, jb, :], op=ALU.mult
+                        )
+                        nc.vector.reduce_sum(out=t2[:, jb : jb + 1], in_=prod[:], axis=AX.X)
+                        nc.vector.tensor_copy(out=s1[:, jb : jb + 1], in_=y[:, a, P : P + 1])
+                    for q in range(DIRECT):
+                        nc.vector.tensor_tensor(out=t2[:], in0=t2[:], in1=sq01[:, q, :], op=ALU.add)
+                    bsum = small("bsum")
+                    nc.vector.tensor_tensor(out=bsum[:], in0=par[:, 0:4], in1=par[:, 8:12], op=ALU.add)
+                    nc.vector.tensor_tensor(out=bsum[:], in0=bsum[:], in1=par[:, 16:20], op=ALU.add)
+                    mean_hh = small("mean_hh")
+                    nc.vector.tensor_scalar(
+                        out=mean_hh[:], in0=s1[:], scalar1=1.0 / B, scalar2=None, op0=ALU.mult
+                    )
+                    msq = small("msq")
+                    nc.vector.tensor_tensor(out=msq[:], in0=mean_hh[:], in1=mean_hh[:], op=ALU.mult)
+                    var_hh = small("var_hh")
+                    nc.vector.scalar_tensor_tensor(
+                        out=var_hh[:], in0=t2[:], scalar=1.0 / B, in1=msq[:], op0=ALU.mult, op1=ALU.subtract
+                    )
+                    nc.vector.tensor_scalar(
+                        out=var_hh[:], in0=var_hh[:], scalar1=0.0, scalar2=EPS, op0=ALU.max, op1=ALU.add
+                    )
+                    rstd_hh = small("rstd_hh")
+                    nc.gpsimd.tensor_tensor(out=rstd_hh[:], in0=var_hh[:], in1=neghalf[:], op=ALU.pow)
+                if ci == 12:
+                    a_hh = small("a_hh")
+                    nc.vector.tensor_tensor(out=a_hh[:], in0=par[:, 12:16], in1=rstd_hh[:], op=ALU.mult)
+                    cst = small("cst")
+                    nc.vector.tensor_tensor(out=cst[:], in0=a_hh[:], in1=mean_hh[:], op=ALU.mult)
+                    nc.vector.tensor_tensor(out=cst[:], in0=bsum[:], in1=cst[:], op=ALU.subtract)
 
-        bsum = small("bsum")
-        nc.vector.tensor_tensor(out=bsum[:], in0=par[:, 0:4], in1=par[:, 8:12], op=ALU.add)
-        nc.vector.tensor_tensor(out=bsum[:], in0=bsum[:], in1=par[:, 16:20], op=ALU.add)
-        nc.vector.tensor_copy(out=gs[:, 0:P], in_=gram[:])
-        nc.vector.reduce_sum(out=gs[:, P : P + 1], in_=hsum[:], axis=AX.X)
-        t2 = small("t2")
-        s1 = small("s1")
-        for pair in range(2):
-            y = psum.tile([P, 2, P + 2], F32, tag="g", bufs=1, name="y")
-            for a in range(2):
-                jb = 2 * pair + a
-                nc.tensor.matmul(
-                    out=y[:, a, :], lhsT=whhT_f[:, jb * P : (jb + 1) * P], rhs=gs[:],
-                    start=True, stop=True,
-                )
-            for a in range(2):
-                jb = 2 * pair + a
-                nc.vector.tensor_tensor(out=prod[:], in0=y[:, a, 0:P], in1=whh_nat[:, jb, :], op=ALU.mult)
-                nc.vector.reduce_sum(out=t2[:, jb : jb + 1], in_=prod[:], axis=AX.X)
-                nc.vector.tensor_copy(out=s1[:, jb : jb + 1], in_=y[:, a, P : P + 1])
-        for ci in range(DIRECT):
-            nc.vector.tensor_tensor(out=t2[:], in0=t2[:], in1=sq01[:, ci, :], op=ALU.add)
-        mean_hh = small("mean_hh")
-        nc.vector.tensor_scalar(out=mean_hh[:], in0=s1[:], scalar1=1.0 / B, scalar2=None, op0=ALU.mult)
-        msq = small("msq")
-        nc.vector.tensor_tensor(out=msq[:], in0=mean_hh[:], in1=mean_hh[:], op=ALU.mult)
-        var_hh = small("var_hh")
-        nc.vector.scalar_tensor_tensor(
-            out=var_hh[:], in0=t2[:], scalar=1.0 / B, in1=msq[:], op0=ALU.mult, op1=ALU.subtract
-        )
-        nc.vector.tensor_scalar(
-            out=var_hh[:], in0=var_hh[:], scalar1=0.0, scalar2=EPS, op0=ALU.max, op1=ALU.add
-        )
-        rstd_hh = small("rstd_hh")
-        nc.gpsimd.tensor_tensor(out=rstd_hh[:], in0=var_hh[:], in1=neghalf[:], op=ALU.pow)
-        a_hh = small("a_hh")
-        nc.vector.tensor_tensor(out=a_hh[:], in0=par[:, 12:16], in1=rstd_hh[:], op=ALU.mult)
-        cst = small("cst")
-        nc.vector.tensor_tensor(out=cst[:], in0=a_hh[:], in1=mean_hh[:], op=ALU.mult)
-        nc.vector.tensor_tensor(out=cst[:], in0=bsum[:], in1=cst[:], op=ALU.subtract)
-
-        mv = keep.tile([P, NB, 2], F32)
+        late = ctx.enter_context(tc.tile_pool(name="late", bufs=3))
+        cT = late.tile([P, B], BF16, tag="cT", bufs=1, name="cT")
+        for jb in range(NB):
+            nc.vector.bn_stats(out=st_ih[:, jb, CH - 1, :], in_=gate[jb][:, cols(CH - 1)])
         for jb in range(NB):
             nc.vector.bn_aggr(out=mv[:, jb, :], in_=st_ih[:, jb, :, :].rearrange("p c s -> p (c s)"))
         ve_ih = small("ve_ih")
@@ -249,81 +351,135 @@ def tile_lstmcell_t_kernel(
         nc.vector.tensor_tensor(out=am[:], in0=a_ih[:], in1=mv[:, :, 0], op=ALU.mult)
         nc.vector.tensor_tensor(out=cst[:], in0=cst[:], in1=am[:], op=ALU.subtract)
 
-        c_nat = {}
-        for ci in range(CH):
-            cols = slice(ci * CW, (ci + 1) * CW)
-            if ci % TPC == 0:
-                cg = ci // TPC
-                c_nat[cg] = cpool.tile([P, HG, H], BF16, tag="cn", bufs=2, name="c_nat")
-                nc.sync.dma_start(out=c_nat[cg][:], in_=cv[:, cg * HG : (cg + 1) * HG, :])
-            ct = psum.tile([P, CW], BF16, tag="tp", bufs=2, name="ct")
-            for t in range(TPC):
-                tt = (ci % TPC) * TPC + t
-                nc.tensor.transpose(ct[:, t * P : (t + 1) * P], c_nat[ci // TPC][:, tt, :], ident_b[:])
-            cT = cpool.tile([P, CW], BF16, tag="cT", bufs=3, name="cT")
-            nc.scalar.copy(out=cT[:], in_=ct[:])
-            for jb in range(NB):
-                if ci < DIRECT:
-                    hh = hh01[:, jb, ci, :]
-                else:
-                    acc = psum.tile([P, CW], F32, tag="mm", bufs=5, name="acc")
-                    nc.tensor.matmul(
-                        out=acc[:], lhsT=whhT_b[:, jb * P : (jb + 1) * P], rhs=hT[:, cols],
-                        start=True, stop=True,
-                    )
-                    hh = acc[:]
-                nc.vector.scalar_tensor_tensor(
-                    out=gate[jb][:, cols], in0=hh, scalar=ratio[:, jb : jb + 1], in1=gate[jb][:, cols],
-                    op0=ALU.mult, op1=ALU.add,
-                )
-                nc.scalar.activation(
-                    out=gate[jb][:, cols], in_=gate[jb][:, cols],
-                    func=(ACT.Tanh if jb == 3 else ACT.Sigmoid),
-                    scale=sc[:, jb : jb + 1], bias=cst[:, jb : jb + 1],
-                )
-            nc.gpsimd.tensor_tensor(out=gate[0][:, cols], in0=gate[0][:, cols], in1=cT[:], op=ALU.mult)
-            nc.gpsimd.tensor_tensor(
-                out=gate[1][:, cols], in0=gate[1][:, cols], in1=gate[3][:, cols], op=ALU.mult
-            )
-            nc.vector.tensor_tensor(
-                out=gate[0][:, cols], in0=gate[0][:, cols], in1=gate[1][:, cols], op=ALU.add
-            )
-            nc.vector.bn_stats(out=st_c[:, ci, :], in_=gate[0][:, cols])
+        def c_transposed(q, tag):
+            ct = transpose_bf16(tag, [c_nat[q // TPC][:, (q % TPC) * TPC + t, :] for t in range(TPC)])
+            nc.scalar.copy(out=cT[:, cols(q)], in_=ct[:])
 
-        mvc = keep.tile([P, 2], F32)
-        nc.vector.bn_aggr(out=mvc[:], in_=st_c[:].rearrange("p c s -> p (c s)"))
+        fill_tags = ("ta", "tb", "th", "g")
+        n_fill = 0
+        for q in range(DIRECT, CH):
+            ht = transpose_bf16(fill_tags[n_fill % 4], [htile(q, t)[:, 0:H] for t in range(TPC)])
+            nc.scalar.copy(out=hT[:, cols(q)], in_=ht[:])
+            n_fill += 1
+            if q - DIRECT < CFILL:
+                c_transposed(q - DIRECT, fill_tags[n_fill % 4])
+                n_fill += 1
+        load_c(2)
+        load_c(3)
+
+        negm0 = small("negm0", 1)
+
+        def gate_block(ci, jb):
+            if ci < DIRECT:
+                hh = hh01[:, jb, ci, :]
+            else:
+                hh = hh_matmul(ci, jb)[:]
+            nc.vector.scalar_tensor_tensor(
+                out=gate[jb][:, cols(ci)], in0=hh, scalar=ratio[:, jb : jb + 1], in1=gate[jb][:, cols(ci)],
+                op0=ALU.mult, op1=ALU.add,
+            )
+            nc.scalar.activation(
+                out=gate[jb][:, cols(ci)], in_=gate[jb][:, cols(ci)],
+                func=(ACT.Tanh if jb == 3 else ACT.Sigmoid),
+                scale=sc[:, jb : jb + 1], bias=cst[:, jb : jb + 1],
+            )
+
+        def cell_add(ci):
+            nc.vector.scalar_tensor_tensor(
+                out=gate[0][:, cols(ci)], in0=gate[0][:, cols(ci)], scalar=1.0, in1=gate[1][:, cols(ci)],
+                op0=ALU.mult, op1=ALU.add, accum_out=csum[:, ci : ci + 1],
+            )
+            if ci == 0:
+                nc.vector.tensor_scalar(
+                    out=negm0[:], in0=csum[:, 0:1], scalar1=-1.0 / CW, scalar2=None, op0=ALU.mult
+                )
+
+        def cell_square(ci):
+            nc.scalar.activation(
+                out=junk[:], in_=gate[0][:, cols(ci)], func=ACT.Square, bias=negm0[:], scale=1.0,
+                accum_out=csq[:, ci : ci + 1],
+            )
+
+        for ci in range(CH):
+            for jb in (0, 1, 3):
+                gate_block(ci, jb)
+            nc.gpsimd.tensor_tensor(
+                out=gate[0][:, cols(ci)], in0=gate[0][:, cols(ci)], in1=cT[:, cols(ci)], op=ALU.mult
+            )
+            nc.gpsimd.tensor_tensor(
+                out=gate[1][:, cols(ci)], in0=gate[1][:, cols(ci)], in1=gate[3][:, cols(ci)], op=ALU.mult
+            )
+            if ci >= OLAG:
+                gate_block(ci - OLAG, 2)
+            if ci >= 2:
+                cell_add(ci - 2)
+            if ci >= 3:
+                cell_square(ci - 3)
+            if ci < CH - CFILL:
+                c_transposed(ci + CFILL, ("ta", "tb")[ci % 2])
+
+        gate_block(CH - 6, 2)
+        cell_add(CH - 2)
+        cell_square(CH - 3)
+        gate_block(CH - 5, 2)
+        gate_block(CH - 4, 2)
+        cell_add(CH - 1)
+        cell_square(CH - 2)
+        cell_square(CH - 1)
+        gate_block(CH - 3, 2)
+        s1c = small("s1c", 1)
+        nc.vector.reduce_sum(out=s1c[:], in_=csum[:], axis=AX.X)
+        mean_c = small("mean_c", 1)
+        nc.vector.tensor_scalar(out=mean_c[:], in0=s1c[:], scalar1=1.0 / B, scalar2=None, op0=ALU.mult)
+        dlt = small("dlt", 1)
+        nc.vector.tensor_tensor(out=dlt[:], in0=mean_c[:], in1=negm0[:], op=ALU.add)
+        nc.vector.tensor_tensor(out=dlt[:], in0=dlt[:], in1=dlt[:], op=ALU.mult)
+        s2c = small("s2c", 1)
+        nc.vector.reduce_sum(out=s2c[:], in_=csq[:], axis=AX.X)
         ve_c = small("ve_c", 1)
-        nc.vector.tensor_scalar(out=ve_c[:], in0=mvc[:, 1:2], scalar1=EPS, scalar2=None, op0=ALU.add)
+        nc.vector.scalar_tensor_tensor(
+            out=ve_c[:], in0=s2c[:], scalar=1.0 / B, in1=dlt[:], op0=ALU.mult, op1=ALU.subtract
+        )
+        nc.vector.tensor_scalar(out=ve_c[:], in0=ve_c[:], scalar1=0.0, scalar2=EPS, op0=ALU.max, op1=ALU.add)
         rstd_c = small("rstd_c", 1)
         nc.gpsimd.tensor_tensor(out=rstd_c[:], in0=ve_c[:], in1=neghalf[:, 0:1], op=ALU.pow)
+        gate_block(CH - 2, 2)
+        gate_block(CH - 1, 2)
         a_c = small("a_c", 1)
         nc.vector.tensor_tensor(out=a_c[:], in0=par[:, 20:21], in1=rstd_c[:], op=ALU.mult)
         k_c = small("k_c", 1)
-        nc.vector.tensor_tensor(out=k_c[:], in0=a_c[:], in1=mvc[:, 0:1], op=ALU.mult)
+        nc.vector.tensor_tensor(out=k_c[:], in0=a_c[:], in1=mean_c[:], op=ALU.mult)
         nc.vector.tensor_tensor(out=k_c[:], in0=par[:, 21:22], in1=k_c[:], op=ALU.subtract)
 
-        with tc.tile_pool(name="outs", bufs=3) as outs:
-            for ci in range(CH):
-                cols = slice(ci * CW, (ci + 1) * CW)
-                nc.vector.tensor_scalar(
-                    out=gate[1][:, cols], in0=gate[0][:, cols], scalar1=a_c[:], scalar2=k_c[:],
+        out_tags = (("ta", "m0", "m2", "g"), ("tb", "m1", "m3", "th"))
+        out_banks = {}
+        LAG = 2
+        for ci in range(CH + LAG):
+            if ci < CH:
+                nc.gpsimd.tensor_scalar(
+                    out=gate[1][:, cols(ci)], in0=gate[0][:, cols(ci)], scalar1=a_c[:], scalar2=k_c[:],
                     op0=ALU.mult, op1=ALU.add,
                 )
                 nc.scalar.activation(
-                    out=gate[3][:, cols], in_=gate[0][:, cols], func=ACT.Tanh, scale=a_c[:], bias=k_c[:]
+                    out=gate[3][:, cols(ci)], in_=gate[0][:, cols(ci)], func=ACT.Tanh,
+                    scale=a_c[:], bias=k_c[:],
                 )
                 nc.vector.tensor_tensor(
-                    out=gate[2][:, cols], in0=gate[2][:, cols], in1=gate[3][:, cols], op=ALU.mult
+                    out=gate[2][:, cols(ci)], in0=gate[2][:, cols(ci)], in1=gate[3][:, cols(ci)], op=ALU.mult
                 )
                 for o, src in enumerate((gate[1], gate[2])):
-                    ot = psum.tile([P, TPC, P], F32, tag="mm", bufs=5, name="ot")
+                    ot = psum.tile([P, TPC, P], F32, tag=out_tags[o][ci % 4], name="ot")
                     for t in range(TPC):
                         nc.tensor.transpose(
                             ot[:, t, :], src[:, ci * CW + t * P : ci * CW + (t + 1) * P], ident_f[:]
                         )
-                    ob = outs.tile([P, TPC, P], F32, tag="ob%d" % o, bufs=3, name="ob")
+                    out_banks[(ci, o)] = ot
+            cj = ci - LAG
+            if cj >= 0:
+                for o in range(2):
+                    ob = late.tile([P, TPC, P], F32, tag="ob%d" % o, bufs=3, name="ob")
                     if o == 0:
-                        nc.scalar.copy(out=ob[:], in_=ot[:])
+                        nc.scalar.copy(out=ob[:], in_=out_banks[(cj, o)][:])
                     else:
-                        nc.vector.tensor_copy(out=ob[:], in_=ot[:])
-                    nc.sync.dma_start(out=outv[o][:, ci * TPC : (ci + 1) * TPC, :], in_=ob[:])
+                        nc.vector.tensor_copy(out=ob[:], in_=out_banks[(cj, o)][:])
+                    nc.sync.dma_start(out=outv[o][:, cj * TPC : (cj + 1) * TPC, :], in_=ob[:])

@@ -24,8 +24,8 @@ DIRECT = 2
 HG = 16
 HPAD = 144
 GW = P + 2
-OLAG = 6
-CFILL = 8
+OLAG = 4
+CFILL = 4
 FLOPS = 2 * B * I * NB * H + 2 * B * H * NB * H
 
 
@@ -61,11 +61,11 @@ def tile_lstmcell_t_kernel(
         par = keep.tile([P, 24], F32)
         gs = keep.tile([P, GW], F32)
         st_ih = keep.tile([P, NB, CH, 6], F32)
-        hsum = keep.tile([P, DIRECT], F32)
+        hsum = keep.tile([P, 1], F32)
         sq01 = keep.tile([P, DIRECT, NB], F32)
         csum = keep.tile([P, CH], F32)
         csq = keep.tile([P, CH], F32)
-        junk = keep.tile([P, CW], BF16)
+        junk = keep.tile([P, 2 * CW], BF16)
         prod = keep.tile([P, P], F32)
         neghalf = keep.tile([P, NB], F32)
         warm = keep.tile([P, 1], F32)
@@ -85,7 +85,7 @@ def tile_lstmcell_t_kernel(
             return h_nat[s // HG][:, s % HG, :]
 
         def transpose_bf16(tag, tiles):
-            bank = psum.tile([P, CW], BF16, tag=tag, name="bt")
+            bank = psum.tile([P, len(tiles) * P], BF16, tag=tag, name="bt")
             for t, src in enumerate(tiles):
                 nc.tensor.transpose(bank[:, t * P : (t + 1) * P], src, ident_b[:])
             return bank
@@ -220,15 +220,16 @@ def tile_lstmcell_t_kernel(
                     evac(nxt, 0, True)
                     if not v_takes_half(nxt):
                         evac(nxt, 1, True)
-                if ci >= 1:
-                    for jb in range(3):
-                        stat_ih(ci - 1, jb)
                 if nxt < CH and v_takes_half(nxt):
                     evac(nxt, 1, False)
                 if ci >= 1:
-                    stat_ih(ci - 1, 3)
+                    stat_ih(ci - 1, 0)
+                    stat_ih(ci - 1, 1)
                 if nxt < CH:
                     quant(nxt)
+                if ci >= 1:
+                    stat_ih(ci - 1, 2)
+                    stat_ih(ci - 1, 3)
                 if ci + 2 < CH:
                     t1(ci + 2, x_sb[ci + 2])
                     if ci + 6 < CH:
@@ -246,11 +247,10 @@ def tile_lstmcell_t_kernel(
                     nc.vector.tensor_copy(out=par[:], in_=pt[:, 0:24])
                 copy_ih(ci)
                 if ci == 1:
-                    for q, tag in enumerate(("th", "g")):
-                        ht = transpose_bf16(tag, [htile(q, t)[:, 0:H] for t in range(TPC)])
-                        nc.scalar.activation(
-                            out=hT[:, cols(q)], in_=ht[:], func=ACT.Copy, accum_out=hsum[:, q : q + 1]
-                        )
+                    ht = transpose_bf16("th", [htile(0, t)[:, 0:H] for t in range(DIRECT * TPC)])
+                    nc.scalar.activation(
+                        out=hT[:, 0 : DIRECT * CW], in_=ht[:], func=ACT.Copy, accum_out=hsum[:]
+                    )
                 if 3 <= ci <= 9:
                     if ci == 3:
                         gram = psum.tile([P, GW], F32, tag="g", name="gram")
@@ -269,16 +269,15 @@ def tile_lstmcell_t_kernel(
                         acc = hh_matmul(q, jb)
                         nc.vector.tensor_copy(out=hh01[:, jb, q, :], in_=acc[:])
                         nc.scalar.activation(
-                            out=junk[:], in_=acc[:], func=ACT.Square, accum_out=sq01[:, q, jb : jb + 1]
+                            out=junk[:, 0:CW], in_=acc[:], func=ACT.Square, accum_out=sq01[:, q, jb : jb + 1]
                         )
                 if nxt < CH:
                     mx(nxt)
                 if ci == 10:
                     nc.vector.tensor_copy(out=gs[:], in_=gram[:])
-                    for q in range(DIRECT):
-                        nc.vector.tensor_tensor(
-                            out=gs[:, P : P + 1], in0=gs[:, P : P + 1], in1=hsum[:, q : q + 1], op=ALU.add
-                        )
+                    nc.vector.tensor_tensor(
+                        out=gs[:, P : P + 1], in0=gs[:, P : P + 1], in1=hsum[:], op=ALU.add
+                    )
                     ys = []
                     for pair, tag in enumerate(("th", "g")):
                         y = psum.tile([P, 2, GW], F32, tag=tag, name="y")
@@ -351,91 +350,129 @@ def tile_lstmcell_t_kernel(
         nc.vector.tensor_tensor(out=am[:], in0=a_ih[:], in1=mv[:, :, 0], op=ALU.mult)
         nc.vector.tensor_tensor(out=cst[:], in0=cst[:], in1=am[:], op=ALU.subtract)
 
-        def c_transposed(q, tag):
-            ct = transpose_bf16(tag, [c_nat[q // TPC][:, (q % TPC) * TPC + t, :] for t in range(TPC)])
-            nc.scalar.copy(out=cT[:, cols(q)], in_=ct[:])
+        def span(c0, n):
+            return slice(c0 * CW, (c0 + n) * CW)
+
+        def c_transposed(pr, tag):
+            tiles = []
+            for t in range(2 * TPC):
+                s = 2 * pr * TPC + t
+                tiles.append(c_nat[s // HG][:, s % HG, :])
+            ct = transpose_bf16(tag, tiles)
+            nc.scalar.copy(out=cT[:, span(2 * pr, 2)], in_=ct[:])
 
         fill_tags = ("ta", "tb", "th", "g")
         n_fill = 0
-        for q in range(DIRECT, CH):
-            ht = transpose_bf16(fill_tags[n_fill % 4], [htile(q, t)[:, 0:H] for t in range(TPC)])
-            nc.scalar.copy(out=hT[:, cols(q)], in_=ht[:])
+        for pr in range(1, CH // 2):
+            ht = transpose_bf16(fill_tags[n_fill % 4], [htile(2 * pr, t)[:, 0:H] for t in range(2 * TPC)])
+            nc.scalar.copy(out=hT[:, span(2 * pr, 2)], in_=ht[:])
             n_fill += 1
-            if q - DIRECT < CFILL:
-                c_transposed(q - DIRECT, fill_tags[n_fill % 4])
+            if pr - 1 < CFILL:
+                c_transposed(pr - 1, fill_tags[n_fill % 4])
                 n_fill += 1
         load_c(2)
         load_c(3)
 
         negm0 = small("negm0", 1)
+        groups2 = [(2 * g, 2) for g in range(7)] + [(14, 1), (15, 1)]
+        NG = len(groups2)
 
-        def gate_block(ci, jb):
-            if ci < DIRECT:
-                hh = hh01[:, jb, ci, :]
+        def combine_group(c0, n, jbs):
+            if c0 < DIRECT:
+                for jb in jbs:
+                    nc.vector.scalar_tensor_tensor(
+                        out=gate[jb][:, span(0, DIRECT)],
+                        in0=hh01[:, jb, :, :].rearrange("p q w -> p (q w)"),
+                        scalar=ratio[:, jb : jb + 1], in1=gate[jb][:, span(0, DIRECT)],
+                        op0=ALU.mult, op1=ALU.add,
+                    )
             else:
-                hh = hh_matmul(ci, jb)[:]
-            nc.vector.scalar_tensor_tensor(
-                out=gate[jb][:, cols(ci)], in0=hh, scalar=ratio[:, jb : jb + 1], in1=gate[jb][:, cols(ci)],
-                op0=ALU.mult, op1=ALU.add,
-            )
+                for ci in range(c0, c0 + n):
+                    for jb in jbs:
+                        acc = hh_matmul(ci, jb)
+                        nc.vector.scalar_tensor_tensor(
+                            out=gate[jb][:, cols(ci)], in0=acc[:], scalar=ratio[:, jb : jb + 1],
+                            in1=gate[jb][:, cols(ci)], op0=ALU.mult, op1=ALU.add,
+                        )
+
+        def activate(c0, n, jb):
             nc.scalar.activation(
-                out=gate[jb][:, cols(ci)], in_=gate[jb][:, cols(ci)],
+                out=gate[jb][:, span(c0, n)], in_=gate[jb][:, span(c0, n)],
                 func=(ACT.Tanh if jb == 3 else ACT.Sigmoid),
                 scale=sc[:, jb : jb + 1], bias=cst[:, jb : jb + 1],
             )
 
-        def cell_add(ci):
-            nc.vector.scalar_tensor_tensor(
-                out=gate[0][:, cols(ci)], in0=gate[0][:, cols(ci)], scalar=1.0, in1=gate[1][:, cols(ci)],
-                op0=ALU.mult, op1=ALU.add, accum_out=csum[:, ci : ci + 1],
+        def o_work(k):
+            c0, n = groups2[k]
+            combine_group(c0, n, (2,))
+            activate(c0, n, 2)
+
+        def forget_product(eng, k):
+            c0, n = groups2[k]
+            eng.tensor_tensor(
+                out=gate[0][:, span(c0, n)], in0=gate[0][:, span(c0, n)], in1=cT[:, span(c0, n)], op=ALU.mult
             )
-            if ci == 0:
+
+        def input_product(k):
+            c0, n = groups2[k]
+            nc.gpsimd.tensor_tensor(
+                out=gate[1][:, span(c0, n)], in0=gate[1][:, span(c0, n)], in1=gate[3][:, span(c0, n)],
+                op=ALU.mult,
+            )
+
+        def cell_add(k):
+            c0, n = groups2[k]
+            nc.vector.scalar_tensor_tensor(
+                out=gate[0][:, span(c0, n)], in0=gate[0][:, span(c0, n)], scalar=1.0,
+                in1=gate[1][:, span(c0, n)], op0=ALU.mult, op1=ALU.add, accum_out=csum[:, k : k + 1],
+            )
+            if k == 0:
                 nc.vector.tensor_scalar(
-                    out=negm0[:], in0=csum[:, 0:1], scalar1=-1.0 / CW, scalar2=None, op0=ALU.mult
+                    out=negm0[:], in0=csum[:, 0:1], scalar1=-1.0 / (n * CW), scalar2=None, op0=ALU.mult
                 )
 
-        def cell_square(ci):
+        def cell_square(k):
+            c0, n = groups2[k]
             nc.scalar.activation(
-                out=junk[:], in_=gate[0][:, cols(ci)], func=ACT.Square, bias=negm0[:], scale=1.0,
-                accum_out=csq[:, ci : ci + 1],
+                out=junk[:, 0 : n * CW], in_=gate[0][:, span(c0, n)], func=ACT.Square, bias=negm0[:],
+                scale=1.0, accum_out=csq[:, k : k + 1],
             )
 
-        for ci in range(CH):
+        for k in range(NG):
+            c0, n = groups2[k]
+            combine_group(c0, n, (0, 1, 3))
             for jb in (0, 1, 3):
-                gate_block(ci, jb)
-            nc.gpsimd.tensor_tensor(
-                out=gate[0][:, cols(ci)], in0=gate[0][:, cols(ci)], in1=cT[:, cols(ci)], op=ALU.mult
-            )
-            nc.gpsimd.tensor_tensor(
-                out=gate[1][:, cols(ci)], in0=gate[1][:, cols(ci)], in1=gate[3][:, cols(ci)], op=ALU.mult
-            )
-            if ci >= OLAG:
-                gate_block(ci - OLAG, 2)
-            if ci >= 2:
-                cell_add(ci - 2)
-            if ci >= 3:
-                cell_square(ci - 3)
-            if ci < CH - CFILL:
-                c_transposed(ci + CFILL, ("ta", "tb")[ci % 2])
+                activate(c0, n, jb)
+            if k < NG - 1:
+                forget_product(nc.gpsimd, k)
+            input_product(k)
+            if k >= OLAG:
+                o_work(k - OLAG)
+            if k >= 2:
+                cell_add(k - 2)
+            if k >= 3:
+                cell_square(k - 3)
+            if k < CH // 2 - CFILL:
+                c_transposed(k + CFILL, ("ta", "tb")[k % 2])
 
-        gate_block(CH - 6, 2)
-        cell_add(CH - 2)
-        cell_square(CH - 3)
-        gate_block(CH - 5, 2)
-        gate_block(CH - 4, 2)
-        cell_add(CH - 1)
-        cell_square(CH - 2)
-        cell_square(CH - 1)
-        gate_block(CH - 3, 2)
+        o_work(NG - 4)
+        cell_square(NG - 3)
+        forget_product(nc.vector, NG - 1)
+        cell_add(NG - 2)
+        cell_square(NG - 2)
+        o_work(NG - 3)
+        cell_add(NG - 1)
+        cell_square(NG - 1)
+        o_work(NG - 2)
         s1c = small("s1c", 1)
-        nc.vector.reduce_sum(out=s1c[:], in_=csum[:], axis=AX.X)
+        nc.vector.reduce_sum(out=s1c[:], in_=csum[:, 0:NG], axis=AX.X)
         mean_c = small("mean_c", 1)
         nc.vector.tensor_scalar(out=mean_c[:], in0=s1c[:], scalar1=1.0 / B, scalar2=None, op0=ALU.mult)
         dlt = small("dlt", 1)
         nc.vector.tensor_tensor(out=dlt[:], in0=mean_c[:], in1=negm0[:], op=ALU.add)
         nc.vector.tensor_tensor(out=dlt[:], in0=dlt[:], in1=dlt[:], op=ALU.mult)
         s2c = small("s2c", 1)
-        nc.vector.reduce_sum(out=s2c[:], in_=csq[:], axis=AX.X)
+        nc.vector.reduce_sum(out=s2c[:], in_=csq[:, 0:NG], axis=AX.X)
         ve_c = small("ve_c", 1)
         nc.vector.scalar_tensor_tensor(
             out=ve_c[:], in0=s2c[:], scalar=1.0 / B, in1=dlt[:], op0=ALU.mult, op1=ALU.subtract
@@ -443,8 +480,7 @@ def tile_lstmcell_t_kernel(
         nc.vector.tensor_scalar(out=ve_c[:], in0=ve_c[:], scalar1=0.0, scalar2=EPS, op0=ALU.max, op1=ALU.add)
         rstd_c = small("rstd_c", 1)
         nc.gpsimd.tensor_tensor(out=rstd_c[:], in0=ve_c[:], in1=neghalf[:, 0:1], op=ALU.pow)
-        gate_block(CH - 2, 2)
-        gate_block(CH - 1, 2)
+        o_work(NG - 1)
         a_c = small("a_c", 1)
         nc.vector.tensor_tensor(out=a_c[:], in0=par[:, 20:21], in1=rstd_c[:], op=ALU.mult)
         k_c = small("k_c", 1)
@@ -453,33 +489,34 @@ def tile_lstmcell_t_kernel(
 
         out_tags = (("ta", "m0", "m2", "g"), ("tb", "m1", "m3", "th"))
         out_banks = {}
-        LAG = 2
-        for ci in range(CH + LAG):
-            if ci < CH:
+        groups3 = [(0, 1), (1, 1)] + [(2 + 2 * g, 2) for g in range(6)] + [(14, 1), (15, 1)]
+        for k in range(len(groups3) + 1):
+            if k < len(groups3):
+                c0, n = groups3[k]
+                sp = span(c0, n)
                 nc.gpsimd.tensor_scalar(
-                    out=gate[1][:, cols(ci)], in0=gate[0][:, cols(ci)], scalar1=a_c[:], scalar2=k_c[:],
+                    out=gate[1][:, sp], in0=gate[0][:, sp], scalar1=a_c[:], scalar2=k_c[:],
                     op0=ALU.mult, op1=ALU.add,
                 )
                 nc.scalar.activation(
-                    out=gate[3][:, cols(ci)], in_=gate[0][:, cols(ci)], func=ACT.Tanh,
-                    scale=a_c[:], bias=k_c[:],
+                    out=gate[3][:, sp], in_=gate[0][:, sp], func=ACT.Tanh, scale=a_c[:], bias=k_c[:]
                 )
-                nc.vector.tensor_tensor(
-                    out=gate[2][:, cols(ci)], in0=gate[2][:, cols(ci)], in1=gate[3][:, cols(ci)], op=ALU.mult
-                )
-                for o, src in enumerate((gate[1], gate[2])):
-                    ot = psum.tile([P, TPC, P], F32, tag=out_tags[o][ci % 4], name="ot")
-                    for t in range(TPC):
-                        nc.tensor.transpose(
-                            ot[:, t, :], src[:, ci * CW + t * P : ci * CW + (t + 1) * P], ident_f[:]
-                        )
-                    out_banks[(ci, o)] = ot
-            cj = ci - LAG
-            if cj >= 0:
-                for o in range(2):
-                    ob = late.tile([P, TPC, P], F32, tag="ob%d" % o, bufs=3, name="ob")
-                    if o == 0:
-                        nc.scalar.copy(out=ob[:], in_=out_banks[(cj, o)][:])
-                    else:
-                        nc.vector.tensor_copy(out=ob[:], in_=out_banks[(cj, o)][:])
-                    nc.sync.dma_start(out=outv[o][:, cj * TPC : (cj + 1) * TPC, :], in_=ob[:])
+                nc.vector.tensor_tensor(out=gate[2][:, sp], in0=gate[2][:, sp], in1=gate[3][:, sp], op=ALU.mult)
+                for ci in range(c0, c0 + n):
+                    for o, src in enumerate((gate[1], gate[2])):
+                        ot = psum.tile([P, TPC, P], F32, tag=out_tags[o][ci % 4], name="ot")
+                        for t in range(TPC):
+                            nc.tensor.transpose(
+                                ot[:, t, :], src[:, ci * CW + t * P : ci * CW + (t + 1) * P], ident_f[:]
+                            )
+                        out_banks[(ci, o)] = ot
+            if k >= 1:
+                c0, n = groups3[k - 1]
+                for cj in range(c0, c0 + n):
+                    for o in range(2):
+                        ob = late.tile([P, TPC, P], F32, tag="ob%d" % o, bufs=3, name="ob")
+                        if o == 0:
+                            nc.scalar.copy(out=ob[:], in_=out_banks[(cj, o)][:])
+                        else:
+                            nc.vector.tensor_copy(out=ob[:], in_=out_banks[(cj, o)][:])
+                        nc.sync.dma_start(out=outv[o][:, cj * TPC : (cj + 1) * TPC, :], in_=ob[:])

@@ -24,8 +24,8 @@ DIRECT = 2
 HG = 16
 HPAD = 144
 GW = P + 2
-OLAG = 4
-CFILL = 4
+OLAG = 6
+CFILL = 8
 FLOPS = 2 * B * I * NB * H + 2 * B * H * NB * H
 
 
@@ -61,11 +61,11 @@ def tile_lstmcell_t_kernel(
         par = keep.tile([P, 24], F32)
         gs = keep.tile([P, GW], F32)
         st_ih = keep.tile([P, NB, CH, 6], F32)
-        hsum = keep.tile([P, 1], F32)
+        hsum = keep.tile([P, DIRECT], F32)
         sq01 = keep.tile([P, DIRECT, NB], F32)
         csum = keep.tile([P, CH], F32)
         csq = keep.tile([P, CH], F32)
-        junk = keep.tile([P, 2 * CW], BF16)
+        junk = keep.tile([P, CW], BF16)
         prod = keep.tile([P, P], F32)
         neghalf = keep.tile([P, NB], F32)
         warm = keep.tile([P, 1], F32)
@@ -85,7 +85,7 @@ def tile_lstmcell_t_kernel(
             return h_nat[s // HG][:, s % HG, :]
 
         def transpose_bf16(tag, tiles):
-            bank = psum.tile([P, len(tiles) * P], BF16, tag=tag, name="bt")
+            bank = psum.tile([P, CW], BF16, tag=tag, name="bt")
             for t, src in enumerate(tiles):
                 nc.tensor.transpose(bank[:, t * P : (t + 1) * P], src, ident_b[:])
             return bank
@@ -247,10 +247,11 @@ def tile_lstmcell_t_kernel(
                     nc.vector.tensor_copy(out=par[:], in_=pt[:, 0:24])
                 copy_ih(ci)
                 if ci == 1:
-                    ht = transpose_bf16("th", [htile(0, t)[:, 0:H] for t in range(DIRECT * TPC)])
-                    nc.scalar.activation(
-                        out=hT[:, 0 : DIRECT * CW], in_=ht[:], func=ACT.Copy, accum_out=hsum[:]
-                    )
+                    for q, tag in enumerate(("th", "g")):
+                        ht = transpose_bf16(tag, [htile(q, t)[:, 0:H] for t in range(TPC)])
+                        nc.scalar.activation(
+                            out=hT[:, cols(q)], in_=ht[:], func=ACT.Copy, accum_out=hsum[:, q : q + 1]
+                        )
                 if 3 <= ci <= 9:
                     if ci == 3:
                         gram = psum.tile([P, GW], F32, tag="g", name="gram")
@@ -269,15 +270,16 @@ def tile_lstmcell_t_kernel(
                         acc = hh_matmul(q, jb)
                         nc.vector.tensor_copy(out=hh01[:, jb, q, :], in_=acc[:])
                         nc.scalar.activation(
-                            out=junk[:, 0:CW], in_=acc[:], func=ACT.Square, accum_out=sq01[:, q, jb : jb + 1]
+                            out=junk[:], in_=acc[:], func=ACT.Square, accum_out=sq01[:, q, jb : jb + 1]
                         )
                 if nxt < CH:
                     mx(nxt)
                 if ci == 10:
                     nc.vector.tensor_copy(out=gs[:], in_=gram[:])
-                    nc.vector.tensor_tensor(
-                        out=gs[:, P : P + 1], in0=gs[:, P : P + 1], in1=hsum[:], op=ALU.add
-                    )
+                    for q in range(DIRECT):
+                        nc.vector.tensor_tensor(
+                            out=gs[:, P : P + 1], in0=gs[:, P : P + 1], in1=hsum[:, q : q + 1], op=ALU.add
+                        )
                     ys = []
                     for pair, tag in enumerate(("th", "g")):
                         y = psum.tile([P, 2, GW], F32, tag=tag, name="y")
@@ -350,129 +352,89 @@ def tile_lstmcell_t_kernel(
         nc.vector.tensor_tensor(out=am[:], in0=a_ih[:], in1=mv[:, :, 0], op=ALU.mult)
         nc.vector.tensor_tensor(out=cst[:], in0=cst[:], in1=am[:], op=ALU.subtract)
 
-        def span(c0, n):
-            return slice(c0 * CW, (c0 + n) * CW)
-
-        def c_transposed(pr, tag):
-            tiles = []
-            for t in range(2 * TPC):
-                s = 2 * pr * TPC + t
-                tiles.append(c_nat[s // HG][:, s % HG, :])
-            ct = transpose_bf16(tag, tiles)
-            nc.scalar.copy(out=cT[:, span(2 * pr, 2)], in_=ct[:])
+        def c_transposed(q, tag):
+            ct = transpose_bf16(tag, [c_nat[q // TPC][:, (q % TPC) * TPC + t, :] for t in range(TPC)])
+            nc.scalar.copy(out=cT[:, cols(q)], in_=ct[:])
 
         fill_tags = ("ta", "tb", "th", "g")
         n_fill = 0
-        for pr in range(1, CH // 2):
-            ht = transpose_bf16(fill_tags[n_fill % 4], [htile(2 * pr, t)[:, 0:H] for t in range(2 * TPC)])
-            nc.scalar.copy(out=hT[:, span(2 * pr, 2)], in_=ht[:])
+        for q in range(DIRECT, CH):
+            ht = transpose_bf16(fill_tags[n_fill % 4], [htile(q, t)[:, 0:H] for t in range(TPC)])
+            nc.scalar.copy(out=hT[:, cols(q)], in_=ht[:])
             n_fill += 1
-            if pr - 1 < CFILL:
-                c_transposed(pr - 1, fill_tags[n_fill % 4])
+            if q - DIRECT < CFILL:
+                c_transposed(q - DIRECT, fill_tags[n_fill % 4])
                 n_fill += 1
         load_c(2)
         load_c(3)
 
         negm0 = small("negm0", 1)
-        groups2 = [(2 * g, 2) for g in range(7)] + [(14, 1), (15, 1)]
-        NG = len(groups2)
 
-        def combine_group(c0, n, jbs):
-            if c0 < DIRECT:
-                for jb in jbs:
-                    nc.vector.scalar_tensor_tensor(
-                        out=gate[jb][:, span(0, DIRECT)],
-                        in0=hh01[:, jb, :, :].rearrange("p q w -> p (q w)"),
-                        scalar=ratio[:, jb : jb + 1], in1=gate[jb][:, span(0, DIRECT)],
-                        op0=ALU.mult, op1=ALU.add,
-                    )
+        def gate_block(ci, jb):
+            if ci < DIRECT:
+                hh = hh01[:, jb, ci, :]
             else:
-                for ci in range(c0, c0 + n):
-                    for jb in jbs:
-                        acc = hh_matmul(ci, jb)
-                        nc.vector.scalar_tensor_tensor(
-                            out=gate[jb][:, cols(ci)], in0=acc[:], scalar=ratio[:, jb : jb + 1],
-                            in1=gate[jb][:, cols(ci)], op0=ALU.mult, op1=ALU.add,
-                        )
-
-        def activate(c0, n, jb):
+                hh = hh_matmul(ci, jb)[:]
+            nc.vector.scalar_tensor_tensor(
+                out=gate[jb][:, cols(ci)], in0=hh, scalar=ratio[:, jb : jb + 1], in1=gate[jb][:, cols(ci)],
+                op0=ALU.mult, op1=ALU.add,
+            )
             nc.scalar.activation(
-                out=gate[jb][:, span(c0, n)], in_=gate[jb][:, span(c0, n)],
+                out=gate[jb][:, cols(ci)], in_=gate[jb][:, cols(ci)],
                 func=(ACT.Tanh if jb == 3 else ACT.Sigmoid),
                 scale=sc[:, jb : jb + 1], bias=cst[:, jb : jb + 1],
             )
 
-        def o_work(k):
-            c0, n = groups2[k]
-            combine_group(c0, n, (2,))
-            activate(c0, n, 2)
-
-        def forget_product(eng, k):
-            c0, n = groups2[k]
-            eng.tensor_tensor(
-                out=gate[0][:, span(c0, n)], in0=gate[0][:, span(c0, n)], in1=cT[:, span(c0, n)], op=ALU.mult
-            )
-
-        def input_product(k):
-            c0, n = groups2[k]
-            nc.gpsimd.tensor_tensor(
-                out=gate[1][:, span(c0, n)], in0=gate[1][:, span(c0, n)], in1=gate[3][:, span(c0, n)],
-                op=ALU.mult,
-            )
-
-        def cell_add(k):
-            c0, n = groups2[k]
+        def cell_add(ci):
             nc.vector.scalar_tensor_tensor(
-                out=gate[0][:, span(c0, n)], in0=gate[0][:, span(c0, n)], scalar=1.0,
-                in1=gate[1][:, span(c0, n)], op0=ALU.mult, op1=ALU.add, accum_out=csum[:, k : k + 1],
+                out=gate[0][:, cols(ci)], in0=gate[0][:, cols(ci)], scalar=1.0, in1=gate[1][:, cols(ci)],
+                op0=ALU.mult, op1=ALU.add, accum_out=csum[:, ci : ci + 1],
             )
-            if k == 0:
+            if ci == 0:
                 nc.vector.tensor_scalar(
-                    out=negm0[:], in0=csum[:, 0:1], scalar1=-1.0 / (n * CW), scalar2=None, op0=ALU.mult
+                    out=negm0[:], in0=csum[:, 0:1], scalar1=-1.0 / CW, scalar2=None, op0=ALU.mult
                 )
 
-        def cell_square(k):
-            c0, n = groups2[k]
+        def cell_square(ci):
             nc.scalar.activation(
-                out=junk[:, 0 : n * CW], in_=gate[0][:, span(c0, n)], func=ACT.Square, bias=negm0[:],
-                scale=1.0, accum_out=csq[:, k : k + 1],
+                out=junk[:], in_=gate[0][:, cols(ci)], func=ACT.Square, bias=negm0[:], scale=1.0,
+                accum_out=csq[:, ci : ci + 1],
             )
 
-        for k in range(NG):
-            c0, n = groups2[k]
-            combine_group(c0, n, (0, 1, 3))
+        for ci in range(CH):
             for jb in (0, 1, 3):
-                activate(c0, n, jb)
-            if k < NG - 1:
-                forget_product(nc.gpsimd, k)
-            input_product(k)
-            if k >= OLAG:
-                o_work(k - OLAG)
-            if k >= 2:
-                cell_add(k - 2)
-            if k >= 3:
-                cell_square(k - 3)
-            if k < CH // 2 - CFILL:
-                c_transposed(k + CFILL, ("ta", "tb")[k % 2])
+                gate_block(ci, jb)
+            nc.gpsimd.tensor_tensor(
+                out=gate[0][:, cols(ci)], in0=gate[0][:, cols(ci)], in1=cT[:, cols(ci)], op=ALU.mult
+            )
+            nc.gpsimd.tensor_tensor(
+                out=gate[1][:, cols(ci)], in0=gate[1][:, cols(ci)], in1=gate[3][:, cols(ci)], op=ALU.mult
+            )
+            if ci >= 2:
+                cell_add(ci - 2)
+            if ci >= 3:
+                cell_square(ci - 3)
+            if ci < CH - CFILL:
+                c_transposed(ci + CFILL, ("ta", "tb")[ci % 2])
 
-        o_work(NG - 4)
-        cell_square(NG - 3)
-        forget_product(nc.vector, NG - 1)
-        cell_add(NG - 2)
-        cell_square(NG - 2)
-        o_work(NG - 3)
-        cell_add(NG - 1)
-        cell_square(NG - 1)
-        o_work(NG - 2)
+        gate_block(0, 2)
+        cell_add(CH - 2)
+        cell_square(CH - 3)
+        gate_block(1, 2)
+        gate_block(2, 2)
+        cell_add(CH - 1)
+        cell_square(CH - 2)
+        cell_square(CH - 1)
+        gate_block(3, 2)
         s1c = small("s1c", 1)
-        nc.vector.reduce_sum(out=s1c[:], in_=csum[:, 0:NG], axis=AX.X)
+        nc.vector.reduce_sum(out=s1c[:], in_=csum[:], axis=AX.X)
         mean_c = small("mean_c", 1)
         nc.vector.tensor_scalar(out=mean_c[:], in0=s1c[:], scalar1=1.0 / B, scalar2=None, op0=ALU.mult)
         dlt = small("dlt", 1)
         nc.vector.tensor_tensor(out=dlt[:], in0=mean_c[:], in1=negm0[:], op=ALU.add)
         nc.vector.tensor_tensor(out=dlt[:], in0=dlt[:], in1=dlt[:], op=ALU.mult)
         s2c = small("s2c", 1)
-        nc.vector.reduce_sum(out=s2c[:], in_=csq[:, 0:NG], axis=AX.X)
+        nc.vector.reduce_sum(out=s2c[:], in_=csq[:], axis=AX.X)
         ve_c = small("ve_c", 1)
         nc.vector.scalar_tensor_tensor(
             out=ve_c[:], in0=s2c[:], scalar=1.0 / B, in1=dlt[:], op0=ALU.mult, op1=ALU.subtract
@@ -480,43 +442,77 @@ def tile_lstmcell_t_kernel(
         nc.vector.tensor_scalar(out=ve_c[:], in0=ve_c[:], scalar1=0.0, scalar2=EPS, op0=ALU.max, op1=ALU.add)
         rstd_c = small("rstd_c", 1)
         nc.gpsimd.tensor_tensor(out=rstd_c[:], in0=ve_c[:], in1=neghalf[:, 0:1], op=ALU.pow)
-        o_work(NG - 1)
+        gate_block(4, 2)
+        gate_block(5, 2)
         a_c = small("a_c", 1)
         nc.vector.tensor_tensor(out=a_c[:], in0=par[:, 20:21], in1=rstd_c[:], op=ALU.mult)
         k_c = small("k_c", 1)
         nc.vector.tensor_tensor(out=k_c[:], in0=a_c[:], in1=mean_c[:], op=ALU.mult)
         nc.vector.tensor_tensor(out=k_c[:], in0=par[:, 21:22], in1=k_c[:], op=ALU.subtract)
 
-        out_tags = (("ta", "m0", "m2", "g"), ("tb", "m1", "m3", "th"))
-        out_banks = {}
-        groups3 = [(0, 1), (1, 1)] + [(2 + 2 * g, 2) for g in range(6)] + [(14, 1), (15, 1)]
-        for k in range(len(groups3) + 1):
-            if k < len(groups3):
-                c0, n = groups3[k]
-                sp = span(c0, n)
-                nc.gpsimd.tensor_scalar(
-                    out=gate[1][:, sp], in0=gate[0][:, sp], scalar1=a_c[:], scalar2=k_c[:],
-                    op0=ALU.mult, op1=ALU.add,
+        c_tags = ("ta", "m0", "g", "m3")
+        o_tags = ("tb", "m1", "th")
+        back = {}
+
+        def turn_back(ci):
+            for key, src, tag in (("c", gate[1], c_tags[ci % 4]), ("o", gate[2], o_tags[ci % 3])):
+                bank = psum.tile([P, CW], F32, tag=tag, name="bk")
+                for t in range(TPC):
+                    nc.tensor.transpose(
+                        bank[:, t * P : (t + 1) * P], src[:, ci * CW + t * P : ci * CW + (t + 1) * P], ident_f[:]
+                    )
+                back[(key, ci)] = bank
+
+        for ci in range(CH):
+            nc.gpsimd.tensor_scalar(
+                out=gate[1][:, cols(ci)], in0=gate[0][:, cols(ci)], scalar1=a_c[:], scalar2=k_c[:],
+                op0=ALU.mult, op1=ALU.add,
+            )
+        o_bank = {}
+
+        def o_matmul(ci):
+            o_bank[ci] = hh_matmul(ci, 2)
+
+        def o_combine(ci):
+            nc.vector.scalar_tensor_tensor(
+                out=gate[2][:, cols(ci)], in0=o_bank[ci][:], scalar=ratio[:, 2:3], in1=gate[2][:, cols(ci)],
+                op0=ALU.mult, op1=ALU.add,
+            )
+
+        def o_activate(ci):
+            nc.scalar.activation(
+                out=gate[2][:, cols(ci)], in_=gate[2][:, cols(ci)], func=ACT.Sigmoid,
+                scale=sc[:, 2:3], bias=cst[:, 2:3],
+            )
+
+        o_matmul(OLAG)
+        for it in range(CH + 3):
+            cj = it + OLAG
+            ci = it - 2
+            if cj < CH:
+                o_combine(cj)
+                if cj + 1 < CH:
+                    o_matmul(cj + 1)
+            if OLAG <= cj - 1 < CH:
+                o_activate(cj - 1)
+            if 0 <= ci < CH:
+                nc.scalar.activation(out=gate[3][:, cols(ci)], in_=back[("c", ci)][:], func=ACT.Tanh)
+            cp = it - 3
+            if cp >= 0:
+                oc = late.tile([P, CW], F32, tag="oc", bufs=3, name="oc")
+                if cp % 2 == 1:
+                    nc.scalar.copy(out=oc[:], in_=back[("c", cp)][:])
+                else:
+                    nc.vector.tensor_copy(out=oc[:], in_=back[("c", cp)][:])
+                nc.sync.dma_start(
+                    out=outv[0][:, cp * TPC : (cp + 1) * TPC, :], in_=oc[:].rearrange("p (t k) -> p t k", k=H)
                 )
-                nc.scalar.activation(
-                    out=gate[3][:, sp], in_=gate[0][:, sp], func=ACT.Tanh, scale=a_c[:], bias=k_c[:]
+                oh = late.tile([P, CW], F32, tag="oh", bufs=3, name="oh")
+                nc.vector.tensor_tensor(
+                    out=oh[:], in0=back[("o", cp)][:], in1=gate[3][:, cols(cp)], op=ALU.mult
                 )
-                nc.vector.tensor_tensor(out=gate[2][:, sp], in0=gate[2][:, sp], in1=gate[3][:, sp], op=ALU.mult)
-                for ci in range(c0, c0 + n):
-                    for o, src in enumerate((gate[1], gate[2])):
-                        ot = psum.tile([P, TPC, P], F32, tag=out_tags[o][ci % 4], name="ot")
-                        for t in range(TPC):
-                            nc.tensor.transpose(
-                                ot[:, t, :], src[:, ci * CW + t * P : ci * CW + (t + 1) * P], ident_f[:]
-                            )
-                        out_banks[(ci, o)] = ot
-            if k >= 1:
-                c0, n = groups3[k - 1]
-                for cj in range(c0, c0 + n):
-                    for o in range(2):
-                        ob = late.tile([P, TPC, P], F32, tag="ob%d" % o, bufs=3, name="ob")
-                        if o == 0:
-                            nc.scalar.copy(out=ob[:], in_=out_banks[(cj, o)][:])
-                        else:
-                            nc.vector.tensor_copy(out=ob[:], in_=out_banks[(cj, o)][:])
-                        nc.sync.dma_start(out=outv[o][:, cj * TPC : (cj + 1) * TPC, :], in_=ob[:])
+                nc.sync.dma_start(
+                    out=outv[1][:, cp * TPC : (cp + 1) * TPC, :], in_=oh[:].rearrange("p (t k) -> p t k", k=H)
+                )
+            if it < CH:
+                turn_back(it)

@@ -174,7 +174,7 @@ def tile_lstmcell_t_kernel(
                 nc.vector.bn_stats(out=st_ih[:, jb, ci, :], in_=gate[jb][:, cols(ci)])
 
             def v_takes_half(ci):
-                return ci % 4 == 1
+                return False
 
             w_sb = stage.tile([P, NB, I], BF16, tag="xs", bufs=4, name="w_sb")
             nc.sync.dma_start(out=w_sb[:], in_=w_ih.rearrange("(jb m) k -> m jb k", m=P))
@@ -196,11 +196,11 @@ def tile_lstmcell_t_kernel(
             load_x(4)
             new_grp("w")
             evac("w", 0, True)
-            evac("w", 1, False)
+            evac("w", 1, True)
             nc.vector.quantize_mx(out=w_codes[:].bitcast(FP8X4), scales=w_scales[:], in_=grp["w"][:])
             new_grp(0)
             evac(0, 0, True)
-            evac(0, 1, False)
+            evac(0, 1, True)
             quant(0)
             t1(1, x_sb[1])
             load_x(5)
@@ -268,7 +268,7 @@ def tile_lstmcell_t_kernel(
                     q = (ci - 2) // 3
                     for jb in range(NB):
                         acc = hh_matmul(q, jb)
-                        nc.vector.tensor_copy(out=hh01[:, jb, q, :], in_=acc[:])
+                        nc.scalar.copy(out=hh01[:, jb, q, :], in_=acc[:])
                         nc.scalar.activation(
                             out=junk[:], in_=acc[:], func=ACT.Square, accum_out=sq01[:, q, jb : jb + 1]
                         )
@@ -410,6 +410,8 @@ def tile_lstmcell_t_kernel(
             nc.gpsimd.tensor_tensor(
                 out=gate[1][:, cols(ci)], in0=gate[1][:, cols(ci)], in1=gate[3][:, cols(ci)], op=ALU.mult
             )
+            if ci >= OLAG:
+                gate_block(ci - OLAG, 2)
             if ci >= 2:
                 cell_add(ci - 2)
             if ci >= 3:
@@ -417,15 +419,15 @@ def tile_lstmcell_t_kernel(
             if ci < CH - CFILL:
                 c_transposed(ci + CFILL, ("ta", "tb")[ci % 2])
 
-        gate_block(0, 2)
+        gate_block(CH - 6, 2)
         cell_add(CH - 2)
         cell_square(CH - 3)
-        gate_block(1, 2)
-        gate_block(2, 2)
+        gate_block(CH - 5, 2)
+        gate_block(CH - 4, 2)
         cell_add(CH - 1)
         cell_square(CH - 2)
         cell_square(CH - 1)
-        gate_block(3, 2)
+        gate_block(CH - 3, 2)
         s1c = small("s1c", 1)
         nc.vector.reduce_sum(out=s1c[:], in_=csum[:], axis=AX.X)
         mean_c = small("mean_c", 1)
@@ -442,77 +444,43 @@ def tile_lstmcell_t_kernel(
         nc.vector.tensor_scalar(out=ve_c[:], in0=ve_c[:], scalar1=0.0, scalar2=EPS, op0=ALU.max, op1=ALU.add)
         rstd_c = small("rstd_c", 1)
         nc.gpsimd.tensor_tensor(out=rstd_c[:], in0=ve_c[:], in1=neghalf[:, 0:1], op=ALU.pow)
-        gate_block(4, 2)
-        gate_block(5, 2)
+        gate_block(CH - 2, 2)
+        gate_block(CH - 1, 2)
         a_c = small("a_c", 1)
         nc.vector.tensor_tensor(out=a_c[:], in0=par[:, 20:21], in1=rstd_c[:], op=ALU.mult)
         k_c = small("k_c", 1)
         nc.vector.tensor_tensor(out=k_c[:], in0=a_c[:], in1=mean_c[:], op=ALU.mult)
         nc.vector.tensor_tensor(out=k_c[:], in0=par[:, 21:22], in1=k_c[:], op=ALU.subtract)
 
-        c_tags = ("ta", "m0", "g", "m3")
-        o_tags = ("tb", "m1", "th")
-        back = {}
-
-        def turn_back(ci):
-            for key, src, tag in (("c", gate[1], c_tags[ci % 4]), ("o", gate[2], o_tags[ci % 3])):
-                bank = psum.tile([P, CW], F32, tag=tag, name="bk")
-                for t in range(TPC):
-                    nc.tensor.transpose(
-                        bank[:, t * P : (t + 1) * P], src[:, ci * CW + t * P : ci * CW + (t + 1) * P], ident_f[:]
-                    )
-                back[(key, ci)] = bank
-
-        for ci in range(CH):
-            nc.gpsimd.tensor_scalar(
-                out=gate[1][:, cols(ci)], in0=gate[0][:, cols(ci)], scalar1=a_c[:], scalar2=k_c[:],
-                op0=ALU.mult, op1=ALU.add,
-            )
-        o_bank = {}
-
-        def o_matmul(ci):
-            o_bank[ci] = hh_matmul(ci, 2)
-
-        def o_combine(ci):
-            nc.vector.scalar_tensor_tensor(
-                out=gate[2][:, cols(ci)], in0=o_bank[ci][:], scalar=ratio[:, 2:3], in1=gate[2][:, cols(ci)],
-                op0=ALU.mult, op1=ALU.add,
-            )
-
-        def o_activate(ci):
-            nc.scalar.activation(
-                out=gate[2][:, cols(ci)], in_=gate[2][:, cols(ci)], func=ACT.Sigmoid,
-                scale=sc[:, 2:3], bias=cst[:, 2:3],
-            )
-
-        o_matmul(OLAG)
-        for it in range(CH + 3):
-            cj = it + OLAG
-            ci = it - 2
-            if cj < CH:
-                o_combine(cj)
-                if cj + 1 < CH:
-                    o_matmul(cj + 1)
-            if OLAG <= cj - 1 < CH:
-                o_activate(cj - 1)
-            if 0 <= ci < CH:
-                nc.scalar.activation(out=gate[3][:, cols(ci)], in_=back[("c", ci)][:], func=ACT.Tanh)
-            cp = it - 3
-            if cp >= 0:
-                oc = late.tile([P, CW], F32, tag="oc", bufs=3, name="oc")
-                if cp % 2 == 1:
-                    nc.scalar.copy(out=oc[:], in_=back[("c", cp)][:])
-                else:
-                    nc.vector.tensor_copy(out=oc[:], in_=back[("c", cp)][:])
-                nc.sync.dma_start(
-                    out=outv[0][:, cp * TPC : (cp + 1) * TPC, :], in_=oc[:].rearrange("p (t k) -> p t k", k=H)
+        out_tags = (("ta", "m0", "m2", "g"), ("tb", "m1", "m3", "th"))
+        out_banks = {}
+        LAG = 2
+        for ci in range(CH + LAG):
+            if ci < CH:
+                nc.gpsimd.tensor_scalar(
+                    out=gate[1][:, cols(ci)], in0=gate[0][:, cols(ci)], scalar1=a_c[:], scalar2=k_c[:],
+                    op0=ALU.mult, op1=ALU.add,
                 )
-                oh = late.tile([P, CW], F32, tag="oh", bufs=3, name="oh")
+                nc.scalar.activation(
+                    out=gate[3][:, cols(ci)], in_=gate[0][:, cols(ci)], func=ACT.Tanh,
+                    scale=a_c[:], bias=k_c[:],
+                )
                 nc.vector.tensor_tensor(
-                    out=oh[:], in0=back[("o", cp)][:], in1=gate[3][:, cols(cp)], op=ALU.mult
+                    out=gate[2][:, cols(ci)], in0=gate[2][:, cols(ci)], in1=gate[3][:, cols(ci)], op=ALU.mult
                 )
-                nc.sync.dma_start(
-                    out=outv[1][:, cp * TPC : (cp + 1) * TPC, :], in_=oh[:].rearrange("p (t k) -> p t k", k=H)
-                )
-            if it < CH:
-                turn_back(it)
+                for o, src in enumerate((gate[1], gate[2])):
+                    ot = psum.tile([P, TPC, P], F32, tag=out_tags[o][ci % 4], name="ot")
+                    for t in range(TPC):
+                        nc.tensor.transpose(
+                            ot[:, t, :], src[:, ci * CW + t * P : ci * CW + (t + 1) * P], ident_f[:]
+                        )
+                    out_banks[(ci, o)] = ot
+            cj = ci - LAG
+            if cj >= 0:
+                for o in range(2):
+                    ob = late.tile([P, TPC, P], F32, tag="ob%d" % o, bufs=3, name="ob")
+                    if o == 0:
+                        nc.scalar.copy(out=ob[:], in_=out_banks[(cj, o)][:])
+                    else:
+                        nc.vector.tensor_copy(out=ob[:], in_=out_banks[(cj, o)][:])
+                    nc.sync.dma_start(out=outv[o][:, cj * TPC : (cj + 1) * TPC, :], in_=ob[:])

from contextlib import ExitStack

import concourse.mybir as mybir
from concourse.masks import make_identity

F32 = mybir.dt.float32
BF16 = mybir.dt.bfloat16
U32 = mybir.dt.uint32
U8 = mybir.dt.uint8
FP8X4 = mybir.dt.float8_e4m3fn_x4
ACT = mybir.ActivationFunctionType
ALU = mybir.AluOpType
AX = mybir.AxisListType

P = 128
B, I, H = 8192, 512, 128
NB = 4
TILES = B // P
TPC = 4
CH = TILES // TPC
CW = TPC * P
EPS = 1e-5
DIRECT = 2
HG = 16
HPAD = 144
GW = P + 2
OLAG = 6
CFILL = 8
FLOPS = 2 * B * I * NB * H + 2 * B * H * NB * H


def tile_lstmcell_t_kernel(
    tc, x, c, h, w_ih, w_hh, b, g_ih, b_ih, g_hh, b_hh, g_c, b_c, out_0, out_1
):
    nc = tc.nc
    xv = x.rearrange("(p s) k -> p s k", s=TILES)
    cv = c.rearrange("(p s) k -> p s k", s=TILES)
    hv = h.rearrange("(p s) k -> p s k", s=TILES)
    outv = (
        out_0.rearrange("(p s) k -> p s k", s=TILES),
        out_1.rearrange("(p s) k -> p s k", s=TILES),
    )
    with ExitStack() as ctx:
        ctx.enter_context(tc.manual_schedule())
        keep = ctx.enter_context(tc.tile_pool(name="keep", bufs=1))
        psum = ctx.enter_context(tc.psum_pool(name="psum", bufs=1))
        cpool = ctx.enter_context(tc.tile_pool(name="cpool", bufs=2))

        gate = [keep.tile([P, B], F32, name="gate%d" % jb) for jb in range(NB)]
        hT = keep.tile([P, B], BF16)
        hh01 = keep.tile([P, NB, DIRECT, CW], F32)
        h_nat = [keep.tile([P, HG, HPAD], BF16, name="h_nat%d" % g) for g in range(TILES // HG)]
        w_codes = keep.tile([P, NB * P], U32, align_bytes=64)
        w_scales = keep.tile([P, NB * P], U8, align_bytes=64)
        whh_nat = keep.tile([P, NB, H], BF16)
        whhT_b = keep.tile([P, NB * P], BF16)
        whhT_f = keep.tile([P, NB * P], F32)
        ident_f = keep.tile([P, P], F32)
        ident_b = keep.tile([P, P], BF16)
        rows = keep.tile([P, P], BF16)
        par = keep.tile([P, 24], F32)
        gs = keep.tile([P, GW], F32)
        st_ih = keep.tile([P, NB, CH, 6], F32)
        hsum = keep.tile([P, DIRECT], F32)
        sq01 = keep.tile([P, DIRECT, NB], F32)
        csum = keep.tile([P, CH], F32)
        csq = keep.tile([P, CH], F32)
        junk = keep.tile([P, CW], BF16)
        prod = keep.tile([P, P], F32)
        neghalf = keep.tile([P, NB], F32)
        warm = keep.tile([P, 1], F32)
        mv = keep.tile([P, NB, 2], F32)

        def small(name, width=NB):
            return keep.tile([P, width], F32, name=name)

        def cols(ci):
            return slice(ci * CW, (ci + 1) * CW)

        def blk(jb):
            return slice(jb * P, (jb + 1) * P)

        def htile(ci, t):
            s = ci * TPC + t
            return h_nat[s // HG][:, s % HG, :]

        def transpose_bf16(tag, tiles):
            bank = psum.tile([P, CW], BF16, tag=tag, name="bt")
            for t, src in enumerate(tiles):
                nc.tensor.transpose(bank[:, t * P : (t + 1) * P], src, ident_b[:])
            return bank

        def hh_matmul(ci, jb):
            acc = psum.tile([P, CW], F32, tag="m%d" % jb, name="acc")
            nc.tensor.matmul(out=acc[:], lhsT=whhT_b[:, blk(jb)], rhs=hT[:, cols(ci)], start=True, stop=True)
            return acc

        nc.vector.memset(warm[:], 0.0)
        nc.scalar.activation(out=warm[:], in_=warm[:], func=ACT.Sigmoid)
        make_identity(nc, ident_f[:])
        make_identity(nc, ident_b[:])
        nc.vector.memset(rows[:], 0.0)
        nc.vector.memset(neghalf[:], -0.5)
        for g in range(TILES // HG):
            nc.vector.memset(h_nat[g][:, :, H:HPAD], 1.0)

        with tc.tile_pool(name="stage", bufs=2) as stage:
            x_sb = {}
            banks = {}
            grp = {}
            codes = {}
            scales = {}
            acc_ih = {}

            def load_x(ci):
                x_sb[ci] = stage.tile([P, TPC, I], BF16, tag="xs", bufs=4, name="x_sb")
                nc.sync.dma_start(out=x_sb[ci][:], in_=xv[:, ci * TPC : (ci + 1) * TPC, :])

            def load_h(g):
                nc.sync.dma_start(out=h_nat[g][:, :, 0:H], in_=hv[:, g * HG : (g + 1) * HG, :])

            def t1(key, src, tags=("ta", "tb")):
                pair = []
                for half, tag in enumerate(tags):
                    xt = psum.tile([P, 2, 2 * P], F32, tag=tag, name="xt")
                    for a in range(2):
                        sw = src[:, 2 * half + a, :].bitcast(F32)
                        for u in range(2):
                            nc.tensor.transpose(
                                xt[:, u, a * P : (a + 1) * P], sw[:, u * P : (u + 1) * P], ident_f[:]
                            )
                    pair.append(xt)
                banks[key] = pair

            def new_grp(key):
                grp[key] = stage.tile([P, 4 * CW], BF16, tag="grp", bufs=2, align_bytes=64, name="grp")

            def evac(key, half, on_scalar):
                words = grp[key][:].bitcast(F32).rearrange("p (r u) -> p r u", u=2)
                dst = words[:, half * 2 * P : (half + 1) * 2 * P, :]
                src = banks[key][half][:].rearrange("p u r -> p r u")
                if on_scalar:
                    nc.scalar.copy(out=dst, in_=src)
                else:
                    nc.vector.tensor_copy(out=dst, in_=src)

            def quant(key):
                codes[key] = stage.tile([P, CW], U32, tag="codes", bufs=2, align_bytes=64, name="codes")
                scales[key] = stage.tile([P, CW], U8, tag="scales", bufs=2, align_bytes=64, name="scales")
                nc.vector.quantize_mx(
                    out=codes[key][:].bitcast(FP8X4), scales=scales[key][:], in_=grp[key][:]
                )

            def mx(ci):
                acc_ih[ci] = []
                for jb in range(NB):
                    acc = psum.tile([P, CW], F32, tag="m%d" % jb, name="acc")
                    nc.tensor.matmul_mx(
                        out=acc[:],
                        lhsT=w_codes[:, blk(jb)].bitcast(FP8X4),
                        lhsT_scale=w_scales[:, blk(jb)],
                        rhs=codes[ci][:].bitcast(FP8X4),
                        rhs_scale=scales[ci][:],
                        start=True,
                        stop=True,
                    )
                    acc_ih[ci].append(acc)

            def copy_ih(ci):
                for jb in range(NB):
                    nc.scalar.copy(out=gate[jb][:, cols(ci)], in_=acc_ih[ci][jb][:])

            def stat_ih(ci, jb):
                nc.vector.bn_stats(out=st_ih[:, jb, ci, :], in_=gate[jb][:, cols(ci)])

            def v_takes_half(ci):
                return False

            w_sb = stage.tile([P, NB, I], BF16, tag="xs", bufs=4, name="w_sb")
            nc.sync.dma_start(out=w_sb[:], in_=w_ih.rearrange("(jb m) k -> m jb k", m=P))
            load_x(0)
            load_x(1)
            load_x(2)
            for v, vec in enumerate((b, g_ih, b_ih, g_hh, b_hh)):
                nc.scalar.dma_start(
                    out=rows[NB * v : NB * (v + 1), :], in_=vec.rearrange("(r m) -> r m", m=P)
                )
            nc.scalar.dma_start(out=rows[20:21, :], in_=g_c.rearrange("(r m) -> r m", m=P))
            nc.scalar.dma_start(out=rows[21:22, :], in_=b_c.rearrange("(r m) -> r m", m=P))
            nc.sync.dma_start(out=whh_nat[:], in_=w_hh.rearrange("(jb m) k -> m jb k", m=P))

            t1("w", w_sb)
            load_x(3)
            load_h(0)
            t1(0, x_sb[0], ("th", "g"))
            load_x(4)
            new_grp("w")
            evac("w", 0, True)
            evac("w", 1, True)
            nc.vector.quantize_mx(out=w_codes[:].bitcast(FP8X4), scales=w_scales[:], in_=grp["w"][:])
            new_grp(0)
            evac(0, 0, True)
            evac(0, 1, True)
            quant(0)
            t1(1, x_sb[1])
            load_x(5)
            mx(0)

            c_nat = {}

            def load_c(cg):
                c_nat[cg] = cpool.tile([P, HG, H], BF16, tag="cn", bufs=2, name="c_nat")
                nc.sync.dma_start(out=c_nat[cg][:], in_=cv[:, cg * HG : (cg + 1) * HG, :])

            gram = None
            for ci in range(CH):
                nxt = ci + 1
                if nxt < CH:
                    new_grp(nxt)
                    evac(nxt, 0, True)
                    if not v_takes_half(nxt):
                        evac(nxt, 1, True)
                if nxt < CH and v_takes_half(nxt):
                    evac(nxt, 1, False)
                if ci >= 1:
                    stat_ih(ci - 1, 0)
                    stat_ih(ci - 1, 1)
                if nxt < CH:
                    quant(nxt)
                if ci >= 1:
                    stat_ih(ci - 1, 2)
                    stat_ih(ci - 1, 3)
                if ci + 2 < CH:
                    t1(ci + 2, x_sb[ci + 2])
                    if ci + 6 < CH:
                        load_x(ci + 6)
                if ci in (0, 2, 4):
                    load_h(ci // 2 + 1)
                if ci in (8, 9):
                    load_c(ci - 8)
                if ci == 0:
                    wt = transpose_bf16("g", [whh_nat[:, jb, :] for jb in range(NB)])
                    nc.vector.tensor_copy(out=whhT_b[:], in_=wt[:])
                    nc.vector.tensor_copy(out=whhT_f[:], in_=wt[:])
                    pt = psum.tile([P, P], BF16, tag="th", name="pt")
                    nc.tensor.transpose(pt[:], rows[:], ident_b[:])
                    nc.vector.tensor_copy(out=par[:], in_=pt[:, 0:24])
                copy_ih(ci)
                if ci == 1:
                    for q, tag in enumerate(("th", "g")):
                        ht = transpose_bf16(tag, [htile(q, t)[:, 0:H] for t in range(TPC)])
                        nc.scalar.activation(
                            out=hT[:, cols(q)], in_=ht[:], func=ACT.Copy, accum_out=hsum[:, q : q + 1]
                        )
                if 3 <= ci <= 9:
                    if ci == 3:
                        gram = psum.tile([P, GW], F32, tag="g", name="gram")
                    for q in (2 * ci - 4, 2 * ci - 3):
                        for t in range(TPC):
                            nc.tensor.matmul(
                                out=gram[:],
                                lhsT=htile(q, t)[:, 0:H],
                                rhs=htile(q, t)[:, 0:GW],
                                start=(q == DIRECT and t == 0),
                                stop=(q == CH - 1 and t == TPC - 1),
                            )
                if ci in (2, 5):
                    q = (ci - 2) // 3
                    for jb in range(NB):
                        acc = hh_matmul(q, jb)
                        nc.scalar.copy(out=hh01[:, jb, q, :], in_=acc[:])
                        nc.scalar.activation(
                            out=junk[:], in_=acc[:], func=ACT.Square, accum_out=sq01[:, q, jb : jb + 1]
                        )
                if nxt < CH:
                    mx(nxt)
                if ci == 10:
                    nc.vector.tensor_copy(out=gs[:], in_=gram[:])
                    for q in range(DIRECT):
                        nc.vector.tensor_tensor(
                            out=gs[:, P : P + 1], in0=gs[:, P : P + 1], in1=hsum[:, q : q + 1], op=ALU.add
                        )
                    ys = []
                    for pair, tag in enumerate(("th", "g")):
                        y = psum.tile([P, 2, GW], F32, tag=tag, name="y")
                        for a in range(2):
                            nc.tensor.matmul(
                                out=y[:, a, :], lhsT=whhT_f[:, blk(2 * pair + a)], rhs=gs[:],
                                start=True, stop=True,
                            )
                        ys.append(y)
                if ci == 11:
                    t2 = small("t2")
                    s1 = small("s1")
                    for jb in range(NB):
                        y = ys[jb // 2]
                        a = jb % 2
                        nc.vector.tensor_tensor(
                            out=prod[:], in0=y[:, a, 0:P], in1=whh_nat[:, jb, :], op=ALU.mult
                        )
                        nc.vector.reduce_sum(out=t2[:, jb : jb + 1], in_=prod[:], axis=AX.X)
                        nc.vector.tensor_copy(out=s1[:, jb : jb + 1], in_=y[:, a, P : P + 1])
                    for q in range(DIRECT):
                        nc.vector.tensor_tensor(out=t2[:], in0=t2[:], in1=sq01[:, q, :], op=ALU.add)
                    bsum = small("bsum")
                    nc.vector.tensor_tensor(out=bsum[:], in0=par[:, 0:4], in1=par[:, 8:12], op=ALU.add)
                    nc.vector.tensor_tensor(out=bsum[:], in0=bsum[:], in1=par[:, 16:20], op=ALU.add)
                    mean_hh = small("mean_hh")
                    nc.vector.tensor_scalar(
                        out=mean_hh[:], in0=s1[:], scalar1=1.0 / B, scalar2=None, op0=ALU.mult
                    )
                    msq = small("msq")
                    nc.vector.tensor_tensor(out=msq[:], in0=mean_hh[:], in1=mean_hh[:], op=ALU.mult)
                    var_hh = small("var_hh")
                    nc.vector.scalar_tensor_tensor(
                        out=var_hh[:], in0=t2[:], scalar=1.0 / B, in1=msq[:], op0=ALU.mult, op1=ALU.subtract
                    )
                    nc.vector.tensor_scalar(
                        out=var_hh[:], in0=var_hh[:], scalar1=0.0, scalar2=EPS, op0=ALU.max, op1=ALU.add
                    )
                    rstd_hh = small("rstd_hh")
                    nc.gpsimd.tensor_tensor(out=rstd_hh[:], in0=var_hh[:], in1=neghalf[:], op=ALU.pow)
                if ci == 12:
                    a_hh = small("a_hh")
                    nc.vector.tensor_tensor(out=a_hh[:], in0=par[:, 12:16], in1=rstd_hh[:], op=ALU.mult)
                    cst = small("cst")
                    nc.vector.tensor_tensor(out=cst[:], in0=a_hh[:], in1=mean_hh[:], op=ALU.mult)
                    nc.vector.tensor_tensor(out=cst[:], in0=bsum[:], in1=cst[:], op=ALU.subtract)

        late = ctx.enter_context(tc.tile_pool(name="late", bufs=3))
        cT = late.tile([P, B], BF16, tag="cT", bufs=1, name="cT")
        for jb in range(NB):
            nc.vector.bn_stats(out=st_ih[:, jb, CH - 1, :], in_=gate[jb][:, cols(CH - 1)])
        for jb in range(NB):
            nc.vector.bn_aggr(out=mv[:, jb, :], in_=st_ih[:, jb, :, :].rearrange("p c s -> p (c s)"))
        ve_ih = small("ve_ih")
        nc.vector.tensor_scalar(out=ve_ih[:], in0=mv[:, :, 1], scalar1=EPS, scalar2=None, op0=ALU.add)
        rstd_ih = small("rstd_ih")
        nc.gpsimd.tensor_tensor(out=rstd_ih[:], in0=ve_ih[:], in1=neghalf[:], op=ALU.pow)
        a_ih = small("a_ih")
        nc.vector.tensor_tensor(out=a_ih[:], in0=par[:, 4:8], in1=rstd_ih[:], op=ALU.mult)
        zfix = small("zfix")
        nc.vector.tensor_scalar(
            out=zfix[:], in0=a_ih[:], scalar1=0.0, scalar2=1e-30, op0=ALU.is_equal, op1=ALU.mult
        )
        sc = small("sc")
        nc.vector.tensor_tensor(out=sc[:], in0=a_ih[:], in1=zfix[:], op=ALU.add)
        ratio = small("ratio")
        nc.vector.reciprocal(out=ratio[:], in_=sc[:])
        nc.vector.tensor_tensor(out=ratio[:], in0=ratio[:], in1=a_hh[:], op=ALU.mult)
        am = small("am")
        nc.vector.tensor_tensor(out=am[:], in0=a_ih[:], in1=mv[:, :, 0], op=ALU.mult)
        nc.vector.tensor_tensor(out=cst[:], in0=cst[:], in1=am[:], op=ALU.subtract)

        def c_transposed(q, tag):
            ct = transpose_bf16(tag, [c_nat[q // TPC][:, (q % TPC) * TPC + t, :] for t in range(TPC)])
            nc.scalar.copy(out=cT[:, cols(q)], in_=ct[:])

        fill_tags = ("ta", "tb", "th", "g")
        n_fill = 0
        for q in range(DIRECT, CH):
            ht = transpose_bf16(fill_tags[n_fill % 4], [htile(q, t)[:, 0:H] for t in range(TPC)])
            nc.scalar.copy(out=hT[:, cols(q)], in_=ht[:])
            n_fill += 1
            if q - DIRECT < CFILL:
                c_transposed(q - DIRECT, fill_tags[n_fill % 4])
                n_fill += 1
        load_c(2)
        load_c(3)

        negm0 = small("negm0", 1)

        def gate_block(ci, jb):
            if ci < DIRECT:
                hh = hh01[:, jb, ci, :]
            else:
                hh = hh_matmul(ci, jb)[:]
            nc.vector.scalar_tensor_tensor(
                out=gate[jb][:, cols(ci)], in0=hh, scalar=ratio[:, jb : jb + 1], in1=gate[jb][:, cols(ci)],
                op0=ALU.mult, op1=ALU.add,
            )
            nc.scalar.activation(
                out=gate[jb][:, cols(ci)], in_=gate[jb][:, cols(ci)],
                func=(ACT.Tanh if jb == 3 else ACT.Sigmoid),
                scale=sc[:, jb : jb + 1], bias=cst[:, jb : jb + 1],
            )

        def cell_add(ci):
            nc.vector.scalar_tensor_tensor(
                out=gate[0][:, cols(ci)], in0=gate[0][:, cols(ci)], scalar=1.0, in1=gate[1][:, cols(ci)],
                op0=ALU.mult, op1=ALU.add, accum_out=csum[:, ci : ci + 1],
            )
            if ci == 0:
                nc.vector.tensor_scalar(
                    out=negm0[:], in0=csum[:, 0:1], scalar1=-1.0 / CW, scalar2=None, op0=ALU.mult
                )

        def cell_square(ci):
            nc.scalar.activation(
                out=junk[:], in_=gate[0][:, cols(ci)], func=ACT.Square, bias=negm0[:], scale=1.0,
                accum_out=csq[:, ci : ci + 1],
            )

        for ci in range(CH):
            for jb in (0, 1, 3):
                gate_block(ci, jb)
            nc.gpsimd.tensor_tensor(
                out=gate[0][:, cols(ci)], in0=gate[0][:, cols(ci)], in1=cT[:, cols(ci)], op=ALU.mult
            )
            nc.gpsimd.tensor_tensor(
                out=gate[1][:, cols(ci)], in0=gate[1][:, cols(ci)], in1=gate[3][:, cols(ci)], op=ALU.mult
            )
            if ci >= OLAG:
                gate_block(ci - OLAG, 2)
            if ci >= 2:
                cell_add(ci - 2)
            if ci >= 3:
                cell_square(ci - 3)
            if ci < CH - CFILL:
                c_transposed(ci + CFILL, ("ta", "tb")[ci % 2])

        gate_block(CH - 6, 2)
        cell_add(CH - 2)
        cell_square(CH - 3)
        gate_block(CH - 5, 2)
        gate_block(CH - 4, 2)
        cell_add(CH - 1)
        cell_square(CH - 2)
        cell_square(CH - 1)
        gate_block(CH - 3, 2)
        s1c = small("s1c", 1)
        nc.vector.reduce_sum(out=s1c[:], in_=csum[:], axis=AX.X)
        mean_c = small("mean_c", 1)
        nc.vector.tensor_scalar(out=mean_c[:], in0=s1c[:], scalar1=1.0 / B, scalar2=None, op0=ALU.mult)
        dlt = small("dlt", 1)
        nc.vector.tensor_tensor(out=dlt[:], in0=mean_c[:], in1=negm0[:], op=ALU.add)
        nc.vector.tensor_tensor(out=dlt[:], in0=dlt[:], in1=dlt[:], op=ALU.mult)
        s2c = small("s2c", 1)
        nc.vector.reduce_sum(out=s2c[:], in_=csq[:], axis=AX.X)
        ve_c = small("ve_c", 1)
        nc.vector.scalar_tensor_tensor(
            out=ve_c[:], in0=s2c[:], scalar=1.0 / B, in1=dlt[:], op0=ALU.mult, op1=ALU.subtract
        )
        nc.vector.tensor_scalar(out=ve_c[:], in0=ve_c[:], scalar1=0.0, scalar2=EPS, op0=ALU.max, op1=ALU.add)
        rstd_c = small("rstd_c", 1)
        nc.gpsimd.tensor_tensor(out=rstd_c[:], in0=ve_c[:], in1=neghalf[:, 0:1], op=ALU.pow)
        gate_block(CH - 2, 2)
        gate_block(CH - 1, 2)
        a_c = small("a_c", 1)
        nc.vector.tensor_tensor(out=a_c[:], in0=par[:, 20:21], in1=rstd_c[:], op=ALU.mult)
        k_c = small("k_c", 1)
        nc.vector.tensor_tensor(out=k_c[:], in0=a_c[:], in1=mean_c[:], op=ALU.mult)
        nc.vector.tensor_tensor(out=k_c[:], in0=par[:, 21:22], in1=k_c[:], op=ALU.subtract)

        out_tags = (("ta", "m0", "m2", "g"), ("tb", "m1", "m3", "th"))
        out_banks = {}
        LAG = 2
        for ci in range(CH + LAG):
            if ci < CH:
                nc.gpsimd.tensor_scalar(
                    out=gate[1][:, cols(ci)], in0=gate[0][:, cols(ci)], scalar1=a_c[:], scalar2=k_c[:],
                    op0=ALU.mult, op1=ALU.add,
                )
                nc.scalar.activation(
                    out=gate[3][:, cols(ci)], in_=gate[0][:, cols(ci)], func=ACT.Tanh,
                    scale=a_c[:], bias=k_c[:],
                )
                nc.vector.tensor_tensor(
                    out=gate[2][:, cols(ci)], in0=gate[2][:, cols(ci)], in1=gate[3][:, cols(ci)], op=ALU.mult
                )
                for o, src in enumerate((gate[1], gate[2])):
                    ot = psum.tile([P, TPC, P], F32, tag=out_tags[o][ci % 4], name="ot")
                    for t in range(TPC):
                        nc.tensor.transpose(
                            ot[:, t, :], src[:, ci * CW + t * P : ci * CW + (t + 1) * P], ident_f[:]
                        )
                    out_banks[(ci, o)] = ot
            cj = ci - LAG
            if cj >= 0:
                for o in range(2):
                    ob = late.tile([P, TPC, P], F32, tag="ob%d" % o, bufs=3, name="ob")
                    if o == 0:
                        nc.scalar.copy(out=ob[:], in_=out_banks[(cj, o)][:])
                    else:
                        nc.vector.tensor_copy(out=ob[:], in_=out_banks[(cj, o)][:])
                    nc.sync.dma_start(out=outv[o][:, cj * TPC : (cj + 1) * TPC, :], in_=ob[:])
